import numpy as np
import ml_dtypes


def mxq(x, axis, fmt="e4m3"):
    dtype, down = {"e4m3": (ml_dtypes.float8_e4m3fn, 7), "e5m2": (ml_dtypes.float8_e5m2, 14)}[fmt]
    v = np.moveaxis(np.asarray(x, np.float32).astype(ml_dtypes.bfloat16).astype(np.float64), axis, -1)
    blocks = v.reshape(v.shape[:-1] + (-1, 32))
    amax = np.abs(blocks).max(-1, keepdims=True)
    byte = np.maximum(np.where(amax > 0, np.frexp(amax)[1] - 1 + 127, 0) - down, 1)
    scale = np.exp2(byte - 127.0)
    codes = (blocks / scale).astype(np.float32).astype(dtype).astype(np.float64)
    return np.moveaxis((codes * scale).reshape(v.shape), -1, axis)


WIDE = False


def mx_kscale(k):
    if not WIDE:
        return np.ones(k)
    levels = np.array([10, -10, 5, -5, 0])
    a = np.random.permutation(np.resize(levels, k // 512 * 4)).reshape(k // 512, 4)
    idx = np.arange(k)
    return np.exp2(a[idx // 512, idx % 128 // 32])


BF16 = ml_dtypes.bfloat16


def bf(x):
    return np.asarray(x, np.float32).astype(BF16)


def f64(x):
    return np.asarray(x).astype(np.float64)


B, N, F_IN, D_OUT, EMB_DIM, H1 = 1, 2048, 512, 128, 16, 4
NEG_INF = -1e9
LN_EPS = 1e-3


def setup_inputs():
    r = np.random.standard_normal
    s = mx_kscale(F_IN)
    adj = (0.3 + 0.4 * np.random.random_sample((N, N))) * (np.random.random_sample((N, N)) < 0.5)
    np.fill_diagonal(adj, 1.0)
    return {"q2": bf(r((B, N, D_OUT)) * 1.6), "k2": bf(r((B, N, D_OUT)) * 1.6), "v2": bf(r((B, N, D_OUT)) * 0.2),
            "adj": bf(adj),
            "x": bf(r((B, N, F_IN)) * s), "proj_w": bf(r((F_IN, D_OUT)) * 0.1 / np.sqrt(F_IN) / s[:, None]),
            "ln_g": bf(1.0 + 0.1 * r(D_OUT)), "ln_b": bf(0.1 * r(D_OUT))}


def reference(q2, k2, v2, adj, x, proj_w, ln_g, ln_b):
    scores = f64(q2) @ f64(k2).transpose(0, 2, 1) / np.sqrt(D_OUT)
    scores = np.where(f64(adj)[None] == 0, NEG_INF, scores)
    e = np.exp(scores - scores.max(-1, keepdims=True))
    h = (mxq(e, 2, "e4m3") @ mxq(f64(v2), 1, "e4m3")) / e.sum(-1, keepdims=True)
    skip = mxq(f64(x), 2, "e4m3") @ mxq(f64(proj_w), 0, "e4m3")
    y = h + skip
    mu = y.mean(-1, keepdims=True)
    var = ((y - mu) ** 2).mean(-1, keepdims=True)
    return (y - mu) / np.sqrt(var + LN_EPS) * f64(ln_g) + f64(ln_b)

@@ -1,0 +1,322 @@
+import math
+from contextlib import ExitStack
+
+import concourse.mybir as mybir
+from concourse.masks import make_identity
+
+F32 = mybir.dt.float32
+BF16 = mybir.dt.bfloat16
+U32 = mybir.dt.uint32
+U8 = mybir.dt.uint8
+FP8X4 = mybir.dt.float8_e4m3fn_x4
+ALU = mybir.AluOpType
+ACT = mybir.ActivationFunctionType
+AXIS = mybir.AxisListType
+
+P = 128
+NODES = 2048
+D = 128
+F_IN = 512
+TILES = NODES // P
+BANK = 512
+BANKS = NODES // BANK
+PACK = 4
+K_PASS = P * PACK
+PASSES = NODES // K_PASS
+LN_EPS = 1e-3
+
+Q_SHRINK = 2.0 ** -34
+SCORE_SCALE = 2.0 ** 34 / math.sqrt(D)
+
+FLOPS = 2 * NODES * NODES * D * 2 + 2 * NODES * F_IN * D
+
+
+def tile_spatialprocessor_pa_kernel(tc, q2, k2, v2, adj, x, proj_w, ln_g, ln_b, out):
+    nc = tc.nc
+
+    q_rows = q2.flatten_outer_dims().rearrange("(p t) d -> p t d", t=TILES)
+    adj_rows = adj.rearrange("(p t) k -> p t k", t=TILES)
+    x_rows = x.flatten_outer_dims().rearrange("(p t) f -> p t f", t=TILES)
+    out_rows = out.flatten_outer_dims().rearrange("(p t) d -> p t d", t=TILES)
+    k_rows = k2.flatten_outer_dims().rearrange("(c p) d -> p c d", p=P)
+    v_rows = v2.flatten_outer_dims().rearrange("(c p) d -> p c d", p=P)
+    w_rows = proj_w.rearrange("(u p e) d -> p u (e d)", u=2, e=2)
+
+    with ExitStack() as stack:
+        keep = stack.enter_context(tc.tile_pool(name="keep", bufs=1))
+        ring = stack.enter_context(tc.tile_pool(name="ring", bufs=3))
+        stats = stack.enter_context(tc.tile_pool(name="stats", bufs=6))
+        psum = stack.enter_context(tc.psum_pool(name="psum", bufs=1))
+
+        ident_bf = keep.tile([P, P], BF16, name="ident_bf")
+        make_identity(nc, ident_bf[:])
+        ident_f32 = keep.tile([P, P], F32, name="ident_f32")
+        make_identity(nc, ident_f32[:])
+        neg_half = keep.tile([P, 1], F32, name="neg_half")
+        nc.gpsimd.memset(neg_half[:], -0.5)
+
+        k_sb = keep.tile([P, TILES, D], BF16, name="k_sb")
+        q_sb = keep.tile([P, TILES, D], BF16, name="q_sb")
+        v_sb = keep.tile([P, TILES, D], BF16, name="v_sb")
+        w_sb = keep.tile([P, 2, 2 * D], BF16, name="w_sb")
+        x_sb = keep.tile([P, TILES, F_IN], BF16, name="x_sb")
+        adj_sb = keep.tile([P, TILES, NODES], BF16, name="adj_sb")
+        gain = keep.tile([P, D], BF16, name="gain")
+        shift = keep.tile([P, D], BF16, name="shift")
+
+        def four(group):
+            return slice(4 * group, 4 * group + 4)
+
+        for group in range(4):
+            nc.sync.dma_start(out=k_sb[:, four(group), :], in_=k_rows[:, four(group), :])
+        nc.sync.dma_start(out=q_sb[:, four(0), :], in_=q_rows[:, four(0), :])
+        nc.sync.dma_start(out=adj_sb[:, 0, :], in_=adj_rows[:, 0, :])
+        for group in range(1, 4):
+            nc.sync.dma_start(out=q_sb[:, four(group), :], in_=q_rows[:, four(group), :])
+        nc.sync.dma_start(out=v_sb[:], in_=v_rows)
+        nc.sync.dma_start(out=w_sb[:], in_=w_rows)
+        nc.sync.dma_start(out=adj_sb[:, 1, :], in_=adj_rows[:, 1, :])
+        nc.sync.dma_start(out=x_sb[:], in_=x_rows)
+        nc.sync.dma_start(out=gain[:], in_=ln_g.partition_broadcast(P))
+        nc.sync.dma_start(out=shift[:], in_=ln_b.partition_broadcast(P))
+        for t in range(2, TILES):
+            nc.sync.dma_start(out=adj_sb[:, t, :], in_=adj_rows[:, t, :])
+
+        kT = keep.tile([D, NODES], BF16, name="kT")
+        qT = keep.tile([D, TILES, P], BF16, name="qT")
+
+        def transpose_keys(group):
+            kT_ps = psum.tile([D, 4, P], BF16, name="kT_ps", tag="scores", bufs=BANKS)
+            for c in range(4):
+                nc.tensor.transpose(kT_ps[:, c, :], k_sb[:, 4 * group + c, :], ident_bf[:])
+            nc.vector.tensor_copy(
+                out=kT[:, BANK * group : BANK * (group + 1)],
+                in_=kT_ps[:].rearrange("d c p -> d (c p)"),
+            )
+
+        def transpose_queries(group):
+            qT_ps = psum.tile([D, 4, P], BF16, name="qT_ps", tag="eT", bufs=2)
+            for c in range(4):
+                nc.tensor.transpose(qT_ps[:, c, :], q_sb[:, 4 * group + c, :], ident_bf[:])
+            nc.scalar.mul(out=qT[:, four(group), :], in_=qT_ps[:], mul=Q_SHRINK)
+
+        v_grouped = keep.tile([P, PASSES, D, PACK], BF16, name="v_grouped", align_bytes=64)
+        v_codes = keep.tile([P, PASSES * D], U32, name="v_codes", align_bytes=64)
+        v_scales = keep.tile([P, PASSES * D], U8, name="v_scales", align_bytes=64)
+        w_grouped = keep.tile([P, D, PACK], BF16, name="w_grouped", align_bytes=64)
+        w_codes = keep.tile([P, D], U32, name="w_codes", align_bytes=64)
+        w_scales = keep.tile([P, D], U8, name="w_scales", align_bytes=64)
+
+        def regroup_weights():
+            nc.scalar.copy(
+                out=v_grouped[:], in_=v_sb[:].rearrange("p (g j) d -> p g d j", j=PACK)
+            )
+            nc.scalar.copy(
+                out=w_grouped[:].rearrange("p d (u e) -> p d u e", e=2),
+                in_=w_sb[:].rearrange("p u (e d) -> p d u e", e=2),
+            )
+
+        def quantise_weights():
+            nc.vector.quantize_mx(
+                out=v_codes[:].bitcast(FP8X4),
+                scales=v_scales[:],
+                in_=v_grouped[:].rearrange("p g d j -> p (g d j)"),
+            )
+            nc.vector.quantize_mx(
+                out=w_codes[:].bitcast(FP8X4),
+                scales=w_scales[:],
+                in_=w_grouped[:].rearrange("p d j -> p (d j)"),
+            )
+
+        live = {}
+
+        def scores(t):
+            for b in range(BANKS):
+                s_ps = psum.tile([P, BANK], F32, name="s_ps", tag="scores", bufs=BANKS)
+                nc.tensor.matmul(
+                    out=s_ps[:],
+                    lhsT=qT[:, t, :],
+                    rhs=kT[:, BANK * b : BANK * (b + 1)],
+                    start=True,
+                    stop=True,
+                )
+                live["s_ps", t, b] = s_ps
+
+        def mask_and_min(t):
+            u = ring.tile([P, NODES], F32, name="u", tag="u")
+            for b in range(BANKS):
+                cols = slice(BANK * b, BANK * (b + 1))
+                nc.vector.scalar_tensor_tensor(
+                    out=u[:, cols],
+                    in0=adj_sb[:, t, cols],
+                    scalar=0.0,
+                    in1=live["s_ps", t, b][:],
+                    op0=ALU.is_equal,
+                    op1=ALU.subtract,
+                )
+            u_min = stats.tile([P, 1], F32, name="u_min", tag="u_min")
+            nc.vector.tensor_reduce(out=u_min[:], in_=u[:], axis=AXIS.X, op=ALU.min)
+            live["u", t] = u
+            live["u_min", t] = u_min
+
+        def exponentials(t):
+            max_score = stats.tile([P, 1], F32, name="max_score", tag="max_score")
+            nc.scalar.mul(out=max_score[:], in_=live["u_min", t][:], mul=SCORE_SCALE)
+            e = ring.tile([P, NODES], BF16, name="e", tag="e")
+            row_sum = stats.tile([P, 1], F32, name="row_sum", tag="row_sum")
+            nc.scalar.activation(
+                out=e[:],
+                in_=live["u", t][:],
+                func=ACT.Exp,
+                bias=max_score[:, 0:1],
+                scale=-SCORE_SCALE,
+                accum_out=row_sum[:],
+            )
+            live["e", t] = e
+            live["row_sum", t] = row_sum
+
+        def transposes(t):
+            e = live["e", t]
+            for half in range(2):
+                eT_ps = psum.tile([P, 2 * PACK, P], BF16, name="eT_ps", tag="eT", bufs=2)
+                for c in range(2 * PACK):
+                    chunk = 2 * PACK * half + c
+                    nc.tensor.transpose(eT_ps[:, c, :], e[:, P * chunk : P * (chunk + 1)], ident_bf[:])
+                live["eT_ps", t, half] = eT_ps
+            x_words = x_sb[:, t, :].bitcast(F32)
+            xT_ps = psum.tile([P, 2, P], F32, name="xT_ps", tag="xT", bufs=1)
+            for u in range(2):
+                nc.tensor.transpose(xT_ps[:, u, :], x_words[:, P * u : P * (u + 1)], ident_f32[:])
+            live["xT_ps", t] = xT_ps
+
+        def regroup(t):
+            e_grouped = ring.tile([P, PASSES, P, PACK], BF16, name="e_grouped", tag="e_grouped", align_bytes=64)
+            for half in range(2):
+                nc.scalar.copy(
+                    out=e_grouped[:, 2 * half : 2 * half + 2, :, :],
+                    in_=live["eT_ps", t, half][:].rearrange("p (g j) q -> p g q j", j=PACK),
+                )
+            x_grouped = ring.tile([P, P, PACK], BF16, name="x_grouped", tag="x_grouped", align_bytes=64)
+            nc.scalar.copy(out=x_grouped[:].bitcast(F32), in_=live["xT_ps", t][:].rearrange("p u q -> p q u"))
+            live["e_grouped", t] = e_grouped
+            live["x_grouped", t] = x_grouped
+
+        def quantise(t):
+            e_codes = ring.tile([P, PASSES * P], U32, name="e_codes", tag="e_codes", align_bytes=64)
+            e_scales = ring.tile([P, PASSES * P], U8, name="e_scales", tag="e_scales", align_bytes=64)
+            nc.vector.quantize_mx(
+                out=e_codes[:].bitcast(FP8X4),
+                scales=e_scales[:],
+                in_=live["e_grouped", t][:].rearrange("p g q j -> p (g q j)"),
+            )
+            x_codes = ring.tile([P, P], U32, name="x_codes", tag="x_codes", align_bytes=64)
+            x_scales = ring.tile([P, P], U8, name="x_scales", tag="x_scales", align_bytes=64)
+            nc.vector.quantize_mx(
+                out=x_codes[:].bitcast(FP8X4),
+                scales=x_scales[:],
+                in_=live["x_grouped", t][:].rearrange("p q j -> p (q j)"),
+            )
+            live["e_mx", t] = (e_codes, e_scales)
+            live["x_mx", t] = (x_codes, x_scales)
+
+        def attend(t):
+            e_codes, e_scales = live["e_mx", t]
+            x_codes, x_scales = live["x_mx", t]
+            acc = psum.tile([P, 2, D], F32, name="acc", tag="acc", bufs=1)
+            for g in range(PASSES):
+                cols = slice(P * g, P * (g + 1))
+                nc.tensor.matmul_mx(
+                    out=acc[:, 0, :],
+                    lhsT=e_codes[:, cols].bitcast(FP8X4),
+                    lhsT_scale=e_scales[:, cols],
+                    rhs=v_codes[:, cols].bitcast(FP8X4),
+                    rhs_scale=v_scales[:, cols],
+                    start=(g == 0),
+                    stop=(g == PASSES - 1),
+                )
+            nc.tensor.matmul_mx(
+                out=acc[:, 1, :],
+                lhsT=x_codes[:].bitcast(FP8X4),
+                lhsT_scale=x_scales[:],
+                rhs=w_codes[:].bitcast(FP8X4),
+                rhs_scale=w_scales[:],
+                start=True,
+                stop=True,
+            )
+            skip = ring.tile([P, D], F32, name="skip", tag="skip")
+            nc.scalar.copy(out=skip[:], in_=acc[:, 1, :])
+            live["acc", t] = acc
+            live["skip", t] = skip
+
+        def add_streams(t):
+            inv_sum = stats.tile([P, 1], F32, name="inv_sum", tag="inv_sum")
+            nc.vector.reciprocal(out=inv_sum[:], in_=live["row_sum", t][:])
+            y = ring.tile([P, D], F32, name="y", tag="y", bufs=3)
+            y_sum = stats.tile([P, 1], F32, name="y_sum", tag="y_sum")
+            nc.vector.scalar_tensor_tensor(
+                out=y[:],
+                in0=live["acc", t][:, 0, :],
+                scalar=inv_sum[:, 0:1],
+                in1=live["skip", t][:],
+                op0=ALU.mult,
+                op1=ALU.add,
+                accum_out=y_sum[:],
+            )
+            live["y", t] = y
+            live["y_sum", t] = y_sum
+
+        def layer_norm(t):
+            y = live["y", t]
+            neg_mean = stats.tile([P, 1], F32, name="neg_mean", tag="neg_mean")
+            nc.gpsimd.tensor_scalar(
+                out=neg_mean[:], in0=live["y_sum", t][:], scalar1=-1.0 / D, scalar2=0.0, op0=ALU.mult, op1=ALU.add
+            )
+            squares = ring.tile([P, D], F32, name="squares", tag="squares")
+            sum_sq = stats.tile([P, 1], F32, name="sum_sq", tag="sum_sq")
+            nc.scalar.activation(
+                out=squares[:], in_=y[:], func=ACT.Square, bias=neg_mean[:, 0:1], scale=1.0, accum_out=sum_sq[:]
+            )
+            var_eps = stats.tile([P, 1], F32, name="var_eps", tag="var_eps")
+            nc.gpsimd.tensor_scalar(
+                out=var_eps[:], in0=sum_sq[:], scalar1=1.0 / D, scalar2=LN_EPS, op0=ALU.mult, op1=ALU.add
+            )
+            inv_std = stats.tile([P, 1], F32, name="inv_std", tag="inv_std")
+            nc.gpsimd.tensor_tensor(out=inv_std[:], in0=var_eps[:], in1=neg_half[:], op=ALU.pow)
+            normed = ring.tile([P, D], F32, name="normed", tag="normed")
+            nc.gpsimd.tensor_scalar(
+                out=normed[:], in0=y[:], scalar1=neg_mean[:, 0:1], scalar2=inv_std[:, 0:1], op0=ALU.add, op1=ALU.mult
+            )
+            scaled = ring.tile([P, D], F32, name="scaled", tag="scaled")
+            nc.gpsimd.tensor_tensor(out=scaled[:], in0=normed[:], in1=gain[:], op=ALU.mult)
+            result = ring.tile([P, D], F32, name="result", tag="result", bufs=3)
+            nc.gpsimd.tensor_tensor(out=result[:], in0=scaled[:], in1=shift[:], op=ALU.add)
+            nc.sync.dma_start(out=out_rows[:, t, :], in_=result[:])
+
+        for group in range(4):
+            transpose_keys(group)
+        transpose_queries(0)
+        scores(0)
+        for group in range(1, 4):
+            transpose_queries(group)
+        regroup_weights()
+
+        for r in range(TILES + 3):
+            if r < TILES:
+                mask_and_min(r)
+            if r + 1 < TILES:
+                scores(r + 1)
+            if 0 <= r - 1 < TILES:
+                transposes(r - 1)
+            if r < TILES:
+                exponentials(r)
+            if r == 0:
+                quantise_weights()
+            if 0 <= r - 1 < TILES:
+                regroup(r - 1)
+            if 0 <= r - 3:
+                add_streams(r - 3)
+            if 0 <= r - 2 < TILES:
+                quantise(r - 2)
+                attend(r - 2)
+            if 0 <= r - 3:
+                layer_norm(r - 3)

@@ -38,8 +38,8 @@ def tile_spatialprocessor_pa_kernel(tc, q2, k2, v2, adj, x, proj_w, ln_g, ln_b, 
     adj_rows = adj.rearrange("(p t) k -> p t k", t=TILES)
     x_rows = x.flatten_outer_dims().rearrange("(p t) f -> p t f", t=TILES)
     out_rows = out.flatten_outer_dims().rearrange("(p t) d -> p t d", t=TILES)
-    k_rows = k2.flatten_outer_dims().rearrange("(c p) d -> p c d", p=P)
-    v_rows = v2.flatten_outer_dims().rearrange("(c p) d -> p c d", p=P)
+    k_rows = k2.flatten_outer_dims().rearrange("(b p j) d -> p b (j d)", p=P, j=4)
+    v_rows = v2.flatten_outer_dims().rearrange("(c p e) d -> p c (e d)", p=P, e=2)
     w_rows = proj_w.rearrange("(u p e) d -> p u (e d)", u=2, e=2)
 
     with ExitStack() as stack:
@@ -54,10 +54,12 @@ def tile_spatialprocessor_pa_kernel(tc, q2, k2, v2, adj, x, proj_w, ln_g, ln_b, 
         make_identity(nc, ident_f32[:])
         neg_half = keep.tile([P, 1], F32, name="neg_half")
         nc.gpsimd.memset(neg_half[:], -0.5)
+        neg_one = keep.tile([P, 1], F32, name="neg_one")
+        nc.gpsimd.memset(neg_one[:], -1.0)
 
-        k_sb = keep.tile([P, TILES, D], BF16, name="k_sb")
+        k_sb = keep.tile([P, BANKS, 4 * D], BF16, name="k_sb")
         q_sb = keep.tile([P, TILES, D], BF16, name="q_sb")
-        v_sb = keep.tile([P, TILES, D], BF16, name="v_sb")
+        v_sb = keep.tile([P, TILES // 2, 2 * D], BF16, name="v_sb")
         w_sb = keep.tile([P, 2, 2 * D], BF16, name="w_sb")
         x_sb = keep.tile([P, TILES, F_IN], BF16, name="x_sb")
         adj_sb = keep.tile([P, TILES, NODES], BF16, name="adj_sb")
@@ -67,38 +69,51 @@ def tile_spatialprocessor_pa_kernel(tc, q2, k2, v2, adj, x, proj_w, ln_g, ln_b, 
         def four(group):
             return slice(4 * group, 4 * group + 4)
 
-        for group in range(4):
-            nc.sync.dma_start(out=k_sb[:, four(group), :], in_=k_rows[:, four(group), :])
+        half = NODES // 2
+        nc.sync.dma_start(out=k_sb[:, 0, :], in_=k_rows[:, 0, :])
         nc.sync.dma_start(out=q_sb[:, four(0), :], in_=q_rows[:, four(0), :])
-        nc.sync.dma_start(out=adj_sb[:, 0, :], in_=adj_rows[:, 0, :])
-        for group in range(1, 4):
-            nc.sync.dma_start(out=q_sb[:, four(group), :], in_=q_rows[:, four(group), :])
+        for b in range(1, BANKS):
+            nc.sync.dma_start(out=k_sb[:, b, :], in_=k_rows[:, b, :])
+        nc.sync.dma_start(out=adj_sb[:, 0, :half], in_=adj_rows[:, 0, :half])
+        nc.sync.dma_start(out=adj_sb[:, 0, half:], in_=adj_rows[:, 0, half:])
         nc.sync.dma_start(out=v_sb[:], in_=v_rows)
         nc.sync.dma_start(out=w_sb[:], in_=w_rows)
         nc.sync.dma_start(out=adj_sb[:, 1, :], in_=adj_rows[:, 1, :])
-        nc.sync.dma_start(out=x_sb[:], in_=x_rows)
-        nc.sync.dma_start(out=gain[:], in_=ln_g.partition_broadcast(P))
-        nc.sync.dma_start(out=shift[:], in_=ln_b.partition_broadcast(P))
-        for t in range(2, TILES):
-            nc.sync.dma_start(out=adj_sb[:, t, :], in_=adj_rows[:, t, :])
+        nc.sync.dma_start(out=x_sb[:, four(0), :], in_=x_rows[:, four(0), :])
+        nc.sync.dma_start(out=q_sb[:, four(1), :], in_=q_rows[:, four(1), :])
+        nc.sync.dma_start(out=adj_sb[:, 2, :], in_=adj_rows[:, 2, :])
+        nc.sync.dma_start(out=adj_sb[:, 3, :], in_=adj_rows[:, 3, :])
+        for group in range(1, 4):
+            nc.sync.dma_start(out=x_sb[:, four(group), :], in_=x_rows[:, four(group), :])
+            if group > 1:
+                nc.sync.dma_start(out=q_sb[:, four(group), :], in_=q_rows[:, four(group), :])
+            for t in range(4 * group, 4 * group + 4):
+                nc.sync.dma_start(out=adj_sb[:, t, :], in_=adj_rows[:, t, :])
+            if group == 1:
+                nc.sync.dma_start(out=gain[:], in_=ln_g.partition_broadcast(P))
+                nc.sync.dma_start(out=shift[:], in_=ln_b.partition_broadcast(P))
 
         kT = keep.tile([D, NODES], BF16, name="kT")
         qT = keep.tile([D, TILES, P], BF16, name="qT")
 
-        def transpose_keys(group):
+        def transpose_keys(b):
             kT_ps = psum.tile([D, 4, P], BF16, name="kT_ps", tag="scores", bufs=BANKS)
-            for c in range(4):
-                nc.tensor.transpose(kT_ps[:, c, :], k_sb[:, 4 * group + c, :], ident_bf[:])
+            for j in range(4):
+                nc.tensor.transpose(kT_ps[:, j, :], k_sb[:, b, D * j : D * (j + 1)], ident_bf[:])
             nc.vector.tensor_copy(
-                out=kT[:, BANK * group : BANK * (group + 1)],
-                in_=kT_ps[:].rearrange("d c p -> d (c p)"),
+                out=kT[:, BANK * b : BANK * (b + 1)].rearrange("d (p j) -> d p j", j=4),
+                in_=kT_ps[:].rearrange("d j p -> d p j"),
             )
 
         def transpose_queries(group):
             qT_ps = psum.tile([D, 4, P], BF16, name="qT_ps", tag="eT", bufs=2)
             for c in range(4):
                 nc.tensor.transpose(qT_ps[:, c, :], q_sb[:, 4 * group + c, :], ident_bf[:])
-            nc.scalar.mul(out=qT[:, four(group), :], in_=qT_ps[:], mul=Q_SHRINK)
+            cuts = (0, 1, 4) if group == 0 else (0, 4)
+            for lo, hi in zip(cuts[:-1], cuts[1:]):
+                nc.scalar.mul(
+                    out=qT[:, 4 * group + lo : 4 * group + hi, :], in_=qT_ps[:, lo:hi, :], mul=Q_SHRINK
+                )
 
         v_grouped = keep.tile([P, PASSES, D, PACK], BF16, name="v_grouped", align_bytes=64)
         v_codes = keep.tile([P, PASSES * D], U32, name="v_codes", align_bytes=64)
@@ -108,9 +123,11 @@ def tile_spatialprocessor_pa_kernel(tc, q2, k2, v2, adj, x, proj_w, ln_g, ln_b, 
         w_scales = keep.tile([P, D], U8, name="w_scales", align_bytes=64)
 
         def regroup_weights():
-            nc.scalar.copy(
-                out=v_grouped[:], in_=v_sb[:].rearrange("p (g j) d -> p g d j", j=PACK)
-            )
+            for g in range(PASSES):
+                nc.scalar.copy(
+                    out=v_grouped[:, g, :, :].rearrange("p d (u e) -> p d u e", e=2),
+                    in_=v_sb[:, 2 * g : 2 * g + 2, :].rearrange("p u (e d) -> p d u e", e=2),
+                )
             nc.scalar.copy(
                 out=w_grouped[:].rearrange("p d (u e) -> p d u e", e=2),
                 in_=w_sb[:].rearrange("p u (e d) -> p d u e", e=2),
@@ -142,7 +159,7 @@ def tile_spatialprocessor_pa_kernel(tc, q2, k2, v2, adj, x, proj_w, ln_g, ln_b, 
                 )
                 live["s_ps", t, b] = s_ps
 
-        def mask_and_min(t):
+        def mask(t):
             u = ring.tile([P, NODES], F32, name="u", tag="u")
             for b in range(BANKS):
                 cols = slice(BANK * b, BANK * (b + 1))
@@ -154,9 +171,11 @@ def tile_spatialprocessor_pa_kernel(tc, q2, k2, v2, adj, x, proj_w, ln_g, ln_b, 
                     op0=ALU.is_equal,
                     op1=ALU.subtract,
                 )
-            u_min = stats.tile([P, 1], F32, name="u_min", tag="u_min")
-            nc.vector.tensor_reduce(out=u_min[:], in_=u[:], axis=AXIS.X, op=ALU.min)
             live["u", t] = u
+
+        def row_min(t):
+            u_min = stats.tile([P, 1], F32, name="u_min", tag="u_min")
+            nc.vector.tensor_reduce(out=u_min[:], in_=live["u", t][:], axis=AXIS.X, op=ALU.min)
             live["u_min", t] = u_min
 
         def exponentials(t):
@@ -175,33 +194,37 @@ def tile_spatialprocessor_pa_kernel(tc, q2, k2, v2, adj, x, proj_w, ln_g, ln_b, 
             live["e", t] = e
             live["row_sum", t] = row_sum
 
-        def transposes(t):
-            e = live["e", t]
-            for half in range(2):
-                eT_ps = psum.tile([P, 2 * PACK, P], BF16, name="eT_ps", tag="eT", bufs=2)
-                for c in range(2 * PACK):
-                    chunk = 2 * PACK * half + c
-                    nc.tensor.transpose(eT_ps[:, c, :], e[:, P * chunk : P * (chunk + 1)], ident_bf[:])
-                live["eT_ps", t, half] = eT_ps
+        def transpose_e(t):
+            e_words = live["e", t][:].bitcast(F32)
+            for h in range(2):
+                eT_ps = psum.tile([P, PACK, P], F32, name="eT_ps", tag="eT", bufs=2)
+                for c in range(PACK):
+                    chunk = PACK * h + c
+                    nc.tensor.transpose(eT_ps[:, c, :], e_words[:, P * chunk : P * (chunk + 1)], ident_f32[:])
+                live["eT_ps", t, h] = eT_ps
+
+        def transpose_x(t):
             x_words = x_sb[:, t, :].bitcast(F32)
             xT_ps = psum.tile([P, 2, P], F32, name="xT_ps", tag="xT", bufs=1)
             for u in range(2):
                 nc.tensor.transpose(xT_ps[:, u, :], x_words[:, P * u : P * (u + 1)], ident_f32[:])
             live["xT_ps", t] = xT_ps
 
-        def regroup(t):
+        def regroup_e(t):
             e_grouped = ring.tile([P, PASSES, P, PACK], BF16, name="e_grouped", tag="e_grouped", align_bytes=64)
-            for half in range(2):
+            for h in range(2):
                 nc.scalar.copy(
-                    out=e_grouped[:, 2 * half : 2 * half + 2, :, :],
-                    in_=live["eT_ps", t, half][:].rearrange("p (g j) q -> p g q j", j=PACK),
+                    out=e_grouped[:, 2 * h : 2 * h + 2, :, :].bitcast(F32),
+                    in_=live["eT_ps", t, h][:].rearrange("p (g u) q -> p g q u", u=2),
                 )
+            live["e_grouped", t] = e_grouped
+
+        def regroup_x(t):
             x_grouped = ring.tile([P, P, PACK], BF16, name="x_grouped", tag="x_grouped", align_bytes=64)
             nc.scalar.copy(out=x_grouped[:].bitcast(F32), in_=live["xT_ps", t][:].rearrange("p u q -> p q u"))
-            live["e_grouped", t] = e_grouped
             live["x_grouped", t] = x_grouped
 
-        def quantise(t):
+        def quantise_e(t):
             e_codes = ring.tile([P, PASSES * P], U32, name="e_codes", tag="e_codes", align_bytes=64)
             e_scales = ring.tile([P, PASSES * P], U8, name="e_scales", tag="e_scales", align_bytes=64)
             nc.vector.quantize_mx(
@@ -209,6 +232,9 @@ def tile_spatialprocessor_pa_kernel(tc, q2, k2, v2, adj, x, proj_w, ln_g, ln_b, 
                 scales=e_scales[:],
                 in_=live["e_grouped", t][:].rearrange("p g q j -> p (g q j)"),
             )
+            live["e_mx", t] = (e_codes, e_scales)
+
+        def quantise_x(t):
             x_codes = ring.tile([P, P], U32, name="x_codes", tag="x_codes", align_bytes=64)
             x_scales = ring.tile([P, P], U8, name="x_scales", tag="x_scales", align_bytes=64)
             nc.vector.quantize_mx(
@@ -216,26 +242,25 @@ def tile_spatialprocessor_pa_kernel(tc, q2, k2, v2, adj, x, proj_w, ln_g, ln_b, 
                 scales=x_scales[:],
                 in_=live["x_grouped", t][:].rearrange("p q j -> p (q j)"),
             )
-            live["e_mx", t] = (e_codes, e_scales)
             live["x_mx", t] = (x_codes, x_scales)
 
-        def attend(t):
+        def attend_pass(t, g):
             e_codes, e_scales = live["e_mx", t]
-            x_codes, x_scales = live["x_mx", t]
-            acc = psum.tile([P, 2, D], F32, name="acc", tag="acc", bufs=1)
-            for g in range(PASSES):
-                cols = slice(P * g, P * (g + 1))
-                nc.tensor.matmul_mx(
-                    out=acc[:, 0, :],
-                    lhsT=e_codes[:, cols].bitcast(FP8X4),
-                    lhsT_scale=e_scales[:, cols],
-                    rhs=v_codes[:, cols].bitcast(FP8X4),
-                    rhs_scale=v_scales[:, cols],
-                    start=(g == 0),
-                    stop=(g == PASSES - 1),
-                )
+            cols = slice(P * g, P * (g + 1))
             nc.tensor.matmul_mx(
-                out=acc[:, 1, :],
+                out=live["acc", t][:, 0, :],
+                lhsT=e_codes[:, cols].bitcast(FP8X4),
+                lhsT_scale=e_scales[:, cols],
+                rhs=v_codes[:, cols].bitcast(FP8X4),
+                rhs_scale=v_scales[:, cols],
+                start=(g == 0),
+                stop=(g == PASSES - 1),
+            )
+
+        def project(t):
+            x_codes, x_scales = live["x_mx", t]
+            nc.tensor.matmul_mx(
+                out=live["acc", t][:, 1, :],
                 lhsT=x_codes[:].bitcast(FP8X4),
                 lhsT_scale=x_scales[:],
                 rhs=w_codes[:].bitcast(FP8X4),
@@ -243,39 +268,52 @@ def tile_spatialprocessor_pa_kernel(tc, q2, k2, v2, adj, x, proj_w, ln_g, ln_b, 
                 start=True,
                 stop=True,
             )
-            skip = ring.tile([P, D], F32, name="skip", tag="skip")
-            nc.scalar.copy(out=skip[:], in_=acc[:, 1, :])
-            live["acc", t] = acc
-            live["skip", t] = skip
 
-        def add_streams(t):
+        def attend(t):
+            live["acc", t] = psum.tile([P, 2, D], F32, name="acc", tag="acc", bufs=1)
+            for g in range(PASSES):
+                attend_pass(t, g)
+            project(t)
             inv_sum = stats.tile([P, 1], F32, name="inv_sum", tag="inv_sum")
-            nc.vector.reciprocal(out=inv_sum[:], in_=live["row_sum", t][:])
-            y = ring.tile([P, D], F32, name="y", tag="y", bufs=3)
-            y_sum = stats.tile([P, 1], F32, name="y_sum", tag="y_sum")
-            nc.vector.scalar_tensor_tensor(
-                out=y[:],
-                in0=live["acc", t][:, 0, :],
-                scalar=inv_sum[:, 0:1],
-                in1=live["skip", t][:],
-                op0=ALU.mult,
-                op1=ALU.add,
-                accum_out=y_sum[:],
-            )
-            live["y", t] = y
-            live["y_sum", t] = y_sum
+            nc.gpsimd.tensor_tensor(out=inv_sum[:], in0=live["row_sum", t][:], in1=neg_one[:], op=ALU.pow)
+            live["inv_sum", t] = inv_sum
 
-        def layer_norm(t):
-            y = live["y", t]
+        def out_of_psum(t):
+            h = ring.tile([P, D], F32, name="h", tag="h")
+            h_sum = stats.tile([P, 1], F32, name="h_sum", tag="h_sum")
+            nc.scalar.activation(
+                out=h[:],
+                in_=live["acc", t][:, 0, :],
+                func=ACT.Copy,
+                scale=live["inv_sum", t][:, 0:1],
+                accum_out=h_sum[:],
+            )
+            skip = ring.tile([P, D], F32, name="skip", tag="skip")
+            skip_sum = stats.tile([P, 1], F32, name="skip_sum", tag="skip_sum")
+            nc.scalar.activation(out=skip[:], in_=live["acc", t][:, 1, :], func=ACT.Copy, accum_out=skip_sum[:])
+            y = ring.tile([P, D], F32, name="y", tag="y")
+            nc.gpsimd.tensor_tensor(out=y[:], in0=h[:], in1=skip[:], op=ALU.add)
             neg_mean = stats.tile([P, 1], F32, name="neg_mean", tag="neg_mean")
             nc.gpsimd.tensor_scalar(
-                out=neg_mean[:], in0=live["y_sum", t][:], scalar1=-1.0 / D, scalar2=0.0, op0=ALU.mult, op1=ALU.add
+                out=neg_mean[:], in0=h_sum[:], scalar1=skip_sum[:, 0:1], scalar2=-1.0 / D, op0=ALU.add, op1=ALU.mult
             )
+            live["y", t] = y
+            live["neg_mean", t] = neg_mean
+
+        def sum_squares(t):
+            y = live["y", t]
+            neg_mean = live["neg_mean", t]
             squares = ring.tile([P, D], F32, name="squares", tag="squares")
             sum_sq = stats.tile([P, 1], F32, name="sum_sq", tag="sum_sq")
             nc.scalar.activation(
                 out=squares[:], in_=y[:], func=ACT.Square, bias=neg_mean[:, 0:1], scale=1.0, accum_out=sum_sq[:]
             )
+            live["sum_sq", t] = sum_sq
+
+        def normalise(t):
+            y = live["y", t]
+            neg_mean = live["neg_mean", t]
+            sum_sq = live["sum_sq", t]
             var_eps = stats.tile([P, 1], F32, name="var_eps", tag="var_eps")
             nc.gpsimd.tensor_scalar(
                 out=var_eps[:], in0=sum_sq[:], scalar1=1.0 / D, scalar2=LN_EPS, op0=ALU.mult, op1=ALU.add
@@ -292,31 +330,184 @@ def tile_spatialprocessor_pa_kernel(tc, q2, k2, v2, adj, x, proj_w, ln_g, ln_b, 
             nc.gpsimd.tensor_tensor(out=result[:], in0=scaled[:], in1=shift[:], op=ALU.add)
             nc.sync.dma_start(out=out_rows[:, t, :], in_=result[:])
 
-        for group in range(4):
-            transpose_keys(group)
+        stack.enter_context(tc.manual_schedule())
+        transpose_keys(0)
         transpose_queries(0)
+        for b in range(1, BANKS):
+            transpose_keys(b)
         scores(0)
-        for group in range(1, 4):
-            transpose_queries(group)
         regroup_weights()
-
-        for r in range(TILES + 3):
-            if r < TILES:
-                mask_and_min(r)
-            if r + 1 < TILES:
+        last = TILES - 1
+        for r in range(TILES):
+            mask(r)
+            if r < last:
                 scores(r + 1)
-            if 0 <= r - 1 < TILES:
-                transposes(r - 1)
-            if r < TILES:
-                exponentials(r)
-            if r == 0:
+            transpose_x(r)
+            if r >= 1:
+                exponentials(r - 1)
+            if r >= 3:
+                sum_squares(r - 3)
+            if r in (2, 6, 10):
+                transpose_queries((r + 2) // 4)
+            if r >= 1:
+                transpose_e(r - 1)
+                regroup_e(r - 1)
+            regroup_x(r)
+            if r == 1:
                 quantise_weights()
-            if 0 <= r - 1 < TILES:
-                regroup(r - 1)
-            if 0 <= r - 3:
-                add_streams(r - 3)
-            if 0 <= r - 2 < TILES:
-                quantise(r - 2)
+            if r >= 2:
+                quantise_e(r - 2)
+                quantise_x(r - 2)
                 attend(r - 2)
-            if 0 <= r - 3:
-                layer_norm(r - 3)
+                out_of_psum(r - 2)
+            if r >= 3:
+                normalise(r - 3)
+            row_min(r)
+
+        t14 = last - 1
+        quantise_e(t14)
+        quantise_x(t14)
+        quantise_x(last)
+        live["acc", t14] = psum.tile([P, 2, D], F32, name="acc", tag="acc", bufs=1)
+        for g in range(PASSES):
+            attend_pass(t14, g)
+        project(t14)
+        live["acc", last] = psum.tile([P, 2, D], F32, name="acc_last", tag="scores", bufs=BANKS)
+        project(last)
+
+        max_score = stats.tile([P, 1], F32, name="max_score", tag="max_score")
+        nc.scalar.mul(out=max_score[:], in_=live["u_min", last][:], mul=SCORE_SCALE)
+        e = ring.tile([P, NODES], BF16, name="e", tag="e")
+        half_sum = stats.tile([P, 2], F32, name="half_sum", tag="half_sum")
+        for h in range(2):
+            cols = slice(NODES // 2 * h, NODES // 2 * (h + 1))
+            nc.scalar.activation(
+                out=e[:, cols],
+                in_=live["u", last][:, cols],
+                func=ACT.Exp,
+                bias=max_score[:, 0:1],
+                scale=-SCORE_SCALE,
+                accum_out=half_sum[:, h : h + 1],
+            )
+        sum_squares(last - 2)
+        normalise(last - 2)
+        e_words = e[:].bitcast(F32)
+        e_grouped = ring.tile([P, PASSES, P, PACK], BF16, name="e_grouped", tag="e_grouped", align_bytes=64)
+        e_codes = ring.tile([P, PASSES * P], U32, name="e_codes", tag="e_codes", align_bytes=64)
+        e_scales = ring.tile([P, PASSES * P], U8, name="e_scales", tag="e_scales", align_bytes=64)
+        live["e_mx", last] = (e_codes, e_scales)
+
+        def last_transposes(g):
+            eT_ps = psum.tile([P, 2, P], F32, name="eT_last", tag="scores", bufs=BANKS)
+            for u in range(2):
+                chunk = 2 * g + u
+                nc.tensor.transpose(eT_ps[:, u, :], e_words[:, P * chunk : P * (chunk + 1)], ident_f32[:])
+            live["eT_ps", last, g] = eT_ps
+
+        def last_regroup(g, copy):
+            copy(
+                out=e_grouped[:, g, :, :].bitcast(F32),
+                in_=live["eT_ps", last, g][:].rearrange("p u q -> p q u"),
+            )
+
+        def last_quantise(g, passes):
+            cols = slice(P * g, P * (g + passes))
+            nc.vector.quantize_mx(
+                out=e_codes[:, cols].bitcast(FP8X4),
+                scales=e_scales[:, cols],
+                in_=e_grouped[:, g : g + passes, :, :].rearrange("p g q j -> p (g q j)"),
+            )
+
+        def skip_out(t):
+            skip = ring.tile([P, D], F32, name="skip", tag="skip")
+            nc.vector.tensor_copy(out=skip[:], in_=live["acc", t][:, 1, :])
+            live["skip", t] = skip
+
+        def invert(t, row_sum):
+            inv_sum = stats.tile([P, 1], F32, name="inv_sum", tag="inv_sum")
+            nc.vector.reciprocal(out=inv_sum[:], in_=row_sum)
+            live["inv_sum", t] = inv_sum
+
+        def add_streams(t):
+            y = ring.tile([P, D], F32, name="y", tag="y")
+            nc.vector.scalar_tensor_tensor(
+                out=y[:],
+                in0=live["acc", t][:, 0, :],
+                scalar=live["inv_sum", t][:, 0:1],
+                in1=live["skip", t][:],
+                op0=ALU.mult,
+                op1=ALU.add,
+            )
+            live["y", t] = y
+
+        def moments(t):
+            parts = stats.tile([P, 6], F32, name="parts", tag="parts")
+            nc.vector.bn_stats(out=parts[:], in_=live["y", t][:])
+            mean_var = stats.tile([P, 2], F32, name="mean_var", tag="mean_var")
+            nc.vector.bn_aggr(out=mean_var[:], in_=parts[:])
+            live["mean_var", t] = mean_var
+
+        def inverse_deviation(t):
+            inv_std = stats.tile([P, 1], F32, name="inv_std", tag="inv_std")
+            nc.scalar.activation(
+                out=inv_std[:],
+                in_=live["mean_var", t][:, 1:2],
+                func=ACT.Abs_reciprocal_sqrt,
+                bias=LN_EPS,
+                scale=1.0,
+            )
+            live["inv_std", t] = inv_std
+
+        def centre(t):
+            centred = ring.tile([P, D], F32, name="centred", tag="normed")
+            nc.vector.scalar_tensor_tensor(
+                out=centred[:],
+                in0=live["y", t][:],
+                scalar=live["mean_var", t][:, 0:1],
+                in1=gain[:],
+                op0=ALU.subtract,
+                op1=ALU.mult,
+            )
+            live["centred", t] = centred
+
+        def finish(t):
+            result = ring.tile([P, D], F32, name="result", tag="result", bufs=3)
+            nc.vector.scalar_tensor_tensor(
+                out=result[:],
+                in0=live["centred", t][:],
+                scalar=live["inv_std", t][:, 0:1],
+                in1=shift[:],
+                op0=ALU.mult,
+                op1=ALU.add,
+            )
+            nc.sync.dma_start(out=out_rows[:, t, :], in_=result[:])
+
+        for g in range(PASSES):
+            last_transposes(g)
+        invert(t14, live["row_sum", t14][:])
+        skip_out(t14)
+        add_streams(t14)
+        skip_out(last)
+        last_regroup(0, nc.vector.tensor_copy)
+        last_regroup(1, nc.vector.tensor_copy)
+        moments(t14)
+        last_quantise(0, 2)
+        attend_pass(last, 0)
+        attend_pass(last, 1)
+        row_sum = stats.tile([P, 1], F32, name="row_sum", tag="row_sum")
+        nc.vector.tensor_tensor(out=row_sum[:], in0=half_sum[:, 0:1], in1=half_sum[:, 1:2], op=ALU.add)
+        last_regroup(3, nc.scalar.copy)
+        inverse_deviation(t14)
+        last_regroup(2, nc.vector.tensor_copy)
+        invert(last, row_sum[:])
+        centre(t14)
+        last_quantise(2, 1)
+        last_quantise(3, 1)
+        attend_pass(last, 2)
+        attend_pass(last, 3)
+        finish(t14)
+        add_streams(last)
+        moments(last)
+        inverse_deviation(last)
+        centre(last)
+        finish(last)

@@ -346,22 +346,26 @@ def tile_spatialprocessor_pa_kernel(tc, q2, k2, v2, adj, x, proj_w, ln_g, ln_b, 
             if r >= 1:
                 exponentials(r - 1)
             if r >= 3:
-                sum_squares(r - 3)
+                out_of_psum(r - 3)
+            regroup_x(r)
             if r in (2, 6, 10):
                 transpose_queries((r + 2) // 4)
+            if r >= 4:
+                sum_squares(r - 4)
+                normalise(r - 4)
             if r >= 1:
                 transpose_e(r - 1)
                 regroup_e(r - 1)
-            regroup_x(r)
             if r == 1:
                 quantise_weights()
             if r >= 2:
                 quantise_e(r - 2)
                 quantise_x(r - 2)
                 attend(r - 2)
-                out_of_psum(r - 2)
-            if r >= 3:
+            if r == last:
+                sum_squares(r - 3)
                 normalise(r - 3)
+                out_of_psum(r - 2)
             row_min(r)
 
         t14 = last - 1

@@ -52,10 +52,8 @@ def tile_spatialprocessor_pa_kernel(tc, q2, k2, v2, adj, x, proj_w, ln_g, ln_b, 
         make_identity(nc, ident_bf[:])
         ident_f32 = keep.tile([P, P], F32, name="ident_f32")
         make_identity(nc, ident_f32[:])
-        neg_half = keep.tile([P, 1], F32, name="neg_half")
+        neg_half = keep.tile([P, 2], F32, name="neg_half")
         nc.gpsimd.memset(neg_half[:], -0.5)
-        neg_one = keep.tile([P, 1], F32, name="neg_one")
-        nc.gpsimd.memset(neg_one[:], -1.0)
 
         k_sb = keep.tile([P, BANKS, 4 * D], BF16, name="k_sb")
         q_sb = keep.tile([P, TILES, D], BF16, name="q_sb")
@@ -182,17 +180,18 @@ def tile_spatialprocessor_pa_kernel(tc, q2, k2, v2, adj, x, proj_w, ln_g, ln_b, 
             max_score = stats.tile([P, 1], F32, name="max_score", tag="max_score")
             nc.scalar.mul(out=max_score[:], in_=live["u_min", t][:], mul=SCORE_SCALE)
             e = ring.tile([P, NODES], BF16, name="e", tag="e")
-            row_sum = stats.tile([P, 1], F32, name="row_sum", tag="row_sum")
+            if t % 2 == 0:
+                live["row_sums", t // 2] = stats.tile([P, 2], F32, name="row_sums", tag="row_sums")
+            row_sum = live["row_sums", t // 2][:, t % 2 : t % 2 + 1]
             nc.scalar.activation(
                 out=e[:],
                 in_=live["u", t][:],
                 func=ACT.Exp,
                 bias=max_score[:, 0:1],
                 scale=-SCORE_SCALE,
-                accum_out=row_sum[:],
+                accum_out=row_sum,
             )
             live["e", t] = e
-            live["row_sum", t] = row_sum
 
         def transpose_e(t):
             e_words = live["e", t][:].bitcast(F32)
@@ -248,7 +247,7 @@ def tile_spatialprocessor_pa_kernel(tc, q2, k2, v2, adj, x, proj_w, ln_g, ln_b, 
             e_codes, e_scales = live["e_mx", t]
             cols = slice(P * g, P * (g + 1))
             nc.tensor.matmul_mx(
-                out=live["acc", t][:, 0, :],
+                out=live["acc", t // 2][:, t % 2, 0, :],
                 lhsT=e_codes[:, cols].bitcast(FP8X4),
                 lhsT_scale=e_scales[:, cols],
                 rhs=v_codes[:, cols].bitcast(FP8X4),
@@ -260,7 +259,7 @@ def tile_spatialprocessor_pa_kernel(tc, q2, k2, v2, adj, x, proj_w, ln_g, ln_b, 
         def project(t):
             x_codes, x_scales = live["x_mx", t]
             nc.tensor.matmul_mx(
-                out=live["acc", t][:, 1, :],
+                out=live["acc", t // 2][:, t % 2, 1, :],
                 lhsT=x_codes[:].bitcast(FP8X4),
                 lhsT_scale=x_scales[:],
                 rhs=w_codes[:].bitcast(FP8X4),
@@ -270,65 +269,90 @@ def tile_spatialprocessor_pa_kernel(tc, q2, k2, v2, adj, x, proj_w, ln_g, ln_b, 
             )
 
         def attend(t):
-            live["acc", t] = psum.tile([P, 2, D], F32, name="acc", tag="acc", bufs=1)
+            if t % 2 == 0:
+                live["acc", t // 2] = psum.tile([P, 2, 2, D], F32, name="acc", tag="acc", bufs=1)
             for g in range(PASSES):
                 attend_pass(t, g)
             project(t)
-            inv_sum = stats.tile([P, 1], F32, name="inv_sum", tag="inv_sum")
-            nc.gpsimd.tensor_tensor(out=inv_sum[:], in0=live["row_sum", t][:], in1=neg_one[:], op=ALU.pow)
-            live["inv_sum", t] = inv_sum
 
-        def out_of_psum(t):
-            h = ring.tile([P, D], F32, name="h", tag="h")
-            h_sum = stats.tile([P, 1], F32, name="h_sum", tag="h_sum")
-            nc.scalar.activation(
-                out=h[:],
-                in_=live["acc", t][:, 0, :],
-                func=ACT.Copy,
-                scale=live["inv_sum", t][:, 0:1],
-                accum_out=h_sum[:],
+        def invert_sums(pair):
+            inv_sums = stats.tile([P, 2], F32, name="inv_sums", tag="inv_sums")
+            nc.vector.reciprocal(out=inv_sums[:], in_=live["row_sums", pair][:])
+            live["inv_sums", pair] = inv_sums
+
+        def out_of_psum(pair):
+            acc = live["acc", pair]
+            h = ring.tile([P, 2, D], F32, name="h", tag="h")
+            skip = ring.tile([P, 2, D], F32, name="skip", tag="skip")
+            h_sums = stats.tile([P, 2], F32, name="h_sums", tag="h_sums")
+            skip_sums = stats.tile([P, 2], F32, name="skip_sums", tag="skip_sums")
+            for i in range(2):
+                nc.scalar.activation(
+                    out=h[:, i, :],
+                    in_=acc[:, i, 0, :],
+                    func=ACT.Copy,
+                    scale=live["inv_sums", pair][:, i : i + 1],
+                    accum_out=h_sums[:, i : i + 1],
+                )
+                nc.scalar.activation(
+                    out=skip[:, i, :], in_=acc[:, i, 1, :], func=ACT.Copy, accum_out=skip_sums[:, i : i + 1]
+                )
+            y_sums = stats.tile([P, 2], F32, name="y_sums", tag="y_sums")
+            nc.gpsimd.tensor_tensor(out=y_sums[:], in0=h_sums[:], in1=skip_sums[:], op=ALU.add)
+            neg_means = stats.tile([P, 2], F32, name="neg_means", tag="neg_means")
+            nc.gpsimd.tensor_scalar(
+                out=neg_means[:], in0=y_sums[:], scalar1=-1.0 / D, scalar2=0.0, op0=ALU.mult, op1=ALU.add
             )
-            skip = ring.tile([P, D], F32, name="skip", tag="skip")
-            skip_sum = stats.tile([P, 1], F32, name="skip_sum", tag="skip_sum")
-            nc.scalar.activation(out=skip[:], in_=live["acc", t][:, 1, :], func=ACT.Copy, accum_out=skip_sum[:])
-            y = ring.tile([P, D], F32, name="y", tag="y")
+            y = ring.tile([P, 2, D], F32, name="y", tag="y")
             nc.gpsimd.tensor_tensor(out=y[:], in0=h[:], in1=skip[:], op=ALU.add)
-            neg_mean = stats.tile([P, 1], F32, name="neg_mean", tag="neg_mean")
-            nc.gpsimd.tensor_scalar(
-                out=neg_mean[:], in0=h_sum[:], scalar1=skip_sum[:, 0:1], scalar2=-1.0 / D, op0=ALU.add, op1=ALU.mult
-            )
-            live["y", t] = y
-            live["neg_mean", t] = neg_mean
+            live["y", pair] = y
+            live["neg_means", pair] = neg_means
 
-        def sum_squares(t):
-            y = live["y", t]
-            neg_mean = live["neg_mean", t]
-            squares = ring.tile([P, D], F32, name="squares", tag="squares")
-            sum_sq = stats.tile([P, 1], F32, name="sum_sq", tag="sum_sq")
-            nc.scalar.activation(
-                out=squares[:], in_=y[:], func=ACT.Square, bias=neg_mean[:, 0:1], scale=1.0, accum_out=sum_sq[:]
-            )
-            live["sum_sq", t] = sum_sq
+        def sum_squares(pair):
+            squares = ring.tile([P, 2, D], F32, name="squares", tag="squares")
+            sums_sq = stats.tile([P, 2], F32, name="sums_sq", tag="sums_sq")
+            for i in range(2):
+                nc.scalar.activation(
+                    out=squares[:, i, :],
+                    in_=live["y", pair][:, i, :],
+                    func=ACT.Square,
+                    bias=live["neg_means", pair][:, i : i + 1],
+                    scale=1.0,
+                    accum_out=sums_sq[:, i : i + 1],
+                )
+            live["sums_sq", pair] = sums_sq
 
-        def normalise(t):
-            y = live["y", t]
-            neg_mean = live["neg_mean", t]
-            sum_sq = live["sum_sq", t]
-            var_eps = stats.tile([P, 1], F32, name="var_eps", tag="var_eps")
+        def normalise(pair):
+            vars_eps = stats.tile([P, 2], F32, name="vars_eps", tag="vars_eps")
             nc.gpsimd.tensor_scalar(
-                out=var_eps[:], in0=sum_sq[:], scalar1=1.0 / D, scalar2=LN_EPS, op0=ALU.mult, op1=ALU.add
+                out=vars_eps[:],
+                in0=live["sums_sq", pair][:],
+                scalar1=1.0 / D,
+                scalar2=LN_EPS,
+                op0=ALU.mult,
+                op1=ALU.add,
             )
-            inv_std = stats.tile([P, 1], F32, name="inv_std", tag="inv_std")
-            nc.gpsimd.tensor_tensor(out=inv_std[:], in0=var_eps[:], in1=neg_half[:], op=ALU.pow)
-            normed = ring.tile([P, D], F32, name="normed", tag="normed")
-            nc.gpsimd.tensor_scalar(
-                out=normed[:], in0=y[:], scalar1=neg_mean[:, 0:1], scalar2=inv_std[:, 0:1], op0=ALU.add, op1=ALU.mult
+            inv_stds = stats.tile([P, 2], F32, name="inv_stds", tag="inv_stds")
+            nc.gpsimd.tensor_tensor(out=inv_stds[:], in0=vars_eps[:], in1=neg_half[:], op=ALU.pow)
+            normed = ring.tile([P, 2, D], F32, name="normed", tag="normed")
+            for i in range(2):
+                nc.gpsimd.tensor_scalar(
+                    out=normed[:, i, :],
+                    in0=live["y", pair][:, i, :],
+                    scalar1=live["neg_means", pair][:, i : i + 1],
+                    scalar2=inv_stds[:, i : i + 1],
+                    op0=ALU.add,
+                    op1=ALU.mult,
+                )
+            scaled = ring.tile([P, 2, D], F32, name="scaled", tag="scaled")
+            nc.gpsimd.tensor_tensor(
+                out=scaled[:], in0=normed[:], in1=gain[:].unsqueeze(1).to_broadcast([P, 2, D]), op=ALU.mult
             )
-            scaled = ring.tile([P, D], F32, name="scaled", tag="scaled")
-            nc.gpsimd.tensor_tensor(out=scaled[:], in0=normed[:], in1=gain[:], op=ALU.mult)
-            result = ring.tile([P, D], F32, name="result", tag="result", bufs=3)
-            nc.gpsimd.tensor_tensor(out=result[:], in0=scaled[:], in1=shift[:], op=ALU.add)
-            nc.sync.dma_start(out=out_rows[:, t, :], in_=result[:])
+            result = ring.tile([P, 2, D], F32, name="result", tag="result", bufs=3)
+            nc.gpsimd.tensor_tensor(
+                out=result[:], in0=scaled[:], in1=shift[:].unsqueeze(1).to_broadcast([P, 2, D]), op=ALU.add
+            )
+            nc.sync.dma_start(out=out_rows[:, 2 * pair : 2 * pair + 2, :], in_=result[:])
 
         stack.enter_context(tc.manual_schedule())
         transpose_keys(0)
@@ -345,38 +369,34 @@ def tile_spatialprocessor_pa_kernel(tc, q2, k2, v2, adj, x, proj_w, ln_g, ln_b, 
             transpose_x(r)
             if r >= 1:
                 exponentials(r - 1)
-            if r >= 3:
-                out_of_psum(r - 3)
+            if r >= 4 and r % 2 == 0:
+                out_of_psum((r - 4) // 2)
+            if r >= 5 and r % 2 == 1:
+                sum_squares((r - 5) // 2)
+                normalise((r - 5) // 2)
             regroup_x(r)
             if r in (2, 6, 10):
                 transpose_queries((r + 2) // 4)
-            if r >= 4:
-                sum_squares(r - 4)
-                normalise(r - 4)
             if r >= 1:
                 transpose_e(r - 1)
                 regroup_e(r - 1)
             if r == 1:
                 quantise_weights()
+            if r >= 3 and r % 2 == 1:
+                invert_sums((r - 3) // 2)
             if r >= 2:
                 quantise_e(r - 2)
                 quantise_x(r - 2)
                 attend(r - 2)
             if r == last:
-                sum_squares(r - 3)
-                normalise(r - 3)
-                out_of_psum(r - 2)
+                out_of_psum((r - 3) // 2)
             row_min(r)
 
         t14 = last - 1
         quantise_e(t14)
         quantise_x(t14)
         quantise_x(last)
-        live["acc", t14] = psum.tile([P, 2, D], F32, name="acc", tag="acc", bufs=1)
-        for g in range(PASSES):
-            attend_pass(t14, g)
-        project(t14)
-        live["acc", last] = psum.tile([P, 2, D], F32, name="acc_last", tag="scores", bufs=BANKS)
+        attend(t14)
         project(last)
 
         max_score = stats.tile([P, 1], F32, name="max_score", tag="max_score")
@@ -393,8 +413,8 @@ def tile_spatialprocessor_pa_kernel(tc, q2, k2, v2, adj, x, proj_w, ln_g, ln_b, 
                 scale=-SCORE_SCALE,
                 accum_out=half_sum[:, h : h + 1],
             )
-        sum_squares(last - 2)
-        normalise(last - 2)
+        sum_squares(last // 2 - 1)
+        normalise(last // 2 - 1)
         e_words = e[:].bitcast(F32)
         e_grouped = ring.tile([P, PASSES, P, PACK], BF16, name="e_grouped", tag="e_grouped", align_bytes=64)
         e_codes = ring.tile([P, PASSES * P], U32, name="e_codes", tag="e_codes", align_bytes=64)
@@ -424,7 +444,7 @@ def tile_spatialprocessor_pa_kernel(tc, q2, k2, v2, adj, x, proj_w, ln_g, ln_b, 
 
         def skip_out(t):
             skip = ring.tile([P, D], F32, name="skip", tag="skip")
-            nc.vector.tensor_copy(out=skip[:], in_=live["acc", t][:, 1, :])
+            nc.vector.tensor_copy(out=skip[:], in_=live["acc", t // 2][:, t % 2, 1, :])
             live["skip", t] = skip
 
         def invert(t, row_sum):
@@ -436,7 +456,7 @@ def tile_spatialprocessor_pa_kernel(tc, q2, k2, v2, adj, x, proj_w, ln_g, ln_b, 
             y = ring.tile([P, D], F32, name="y", tag="y")
             nc.vector.scalar_tensor_tensor(
                 out=y[:],
-                in0=live["acc", t][:, 0, :],
+                in0=live["acc", t // 2][:, t % 2, 0, :],
                 scalar=live["inv_sum", t][:, 0:1],
                 in1=live["skip", t][:],
                 op0=ALU.mult,
@@ -475,7 +495,7 @@ def tile_spatialprocessor_pa_kernel(tc, q2, k2, v2, adj, x, proj_w, ln_g, ln_b, 
             live["centred", t] = centred
 
         def finish(t):
-            result = ring.tile([P, D], F32, name="result", tag="result", bufs=3)
+            result = ring.tile([P, D], F32, name="result_last", tag="result", bufs=3)
             nc.vector.scalar_tensor_tensor(
                 out=result[:],
                 in0=live["centred", t][:],
@@ -488,7 +508,7 @@ def tile_spatialprocessor_pa_kernel(tc, q2, k2, v2, adj, x, proj_w, ln_g, ln_b, 
 
         for g in range(PASSES):
             last_transposes(g)
-        invert(t14, live["row_sum", t14][:])
+        invert(t14, live["row_sums", t14 // 2][:, 0:1])
         skip_out(t14)
         add_streams(t14)
         skip_out(last)

@@ -23,9 +23,10 @@ BANKS = NODES // BANK
 PACK = 4
 K_PASS = P * PACK
 PASSES = NODES // K_PASS
+AWAY = BANKS - 1
 LN_EPS = 1e-3
 
-Q_SHRINK = 2.0 ** -34
+K_SHRINK = 2.0 ** -34
 SCORE_SCALE = 2.0 ** 34 / math.sqrt(D)
 
 FLOPS = 2 * NODES * NODES * D * 2 + 2 * NODES * F_IN * D
@@ -98,9 +99,12 @@ def tile_spatialprocessor_pa_kernel(tc, q2, k2, v2, adj, x, proj_w, ln_g, ln_b, 
             kT_ps = psum.tile([D, 4, P], BF16, name="kT_ps", tag="scores", bufs=BANKS)
             for j in range(4):
                 nc.tensor.transpose(kT_ps[:, j, :], k_sb[:, b, D * j : D * (j + 1)], ident_bf[:])
-            nc.vector.tensor_copy(
+            nc.vector.tensor_scalar(
                 out=kT[:, BANK * b : BANK * (b + 1)].rearrange("d (p j) -> d p j", j=4),
-                in_=kT_ps[:].rearrange("d j p -> d p j"),
+                in0=kT_ps[:].rearrange("d j p -> d p j"),
+                scalar1=K_SHRINK,
+                scalar2=None,
+                op0=ALU.mult,
             )
 
         def transpose_queries(group):
@@ -109,9 +113,7 @@ def tile_spatialprocessor_pa_kernel(tc, q2, k2, v2, adj, x, proj_w, ln_g, ln_b, 
                 nc.tensor.transpose(qT_ps[:, c, :], q_sb[:, 4 * group + c, :], ident_bf[:])
             cuts = (0, 1, 4) if group == 0 else (0, 4)
             for lo, hi in zip(cuts[:-1], cuts[1:]):
-                nc.scalar.mul(
-                    out=qT[:, 4 * group + lo : 4 * group + hi, :], in_=qT_ps[:, lo:hi, :], mul=Q_SHRINK
-                )
+                nc.scalar.copy(out=qT[:, 4 * group + lo : 4 * group + hi, :], in_=qT_ps[:, lo:hi, :])
 
         v_grouped = keep.tile([P, PASSES, D, PACK], BF16, name="v_grouped", align_bytes=64)
         v_codes = keep.tile([P, PASSES * D], U32, name="v_codes", align_bytes=64)
@@ -145,8 +147,8 @@ def tile_spatialprocessor_pa_kernel(tc, q2, k2, v2, adj, x, proj_w, ln_g, ln_b, 
 
         live = {}
 
-        def scores(t):
-            for b in range(BANKS):
+        def scores(t, banks):
+            for b in banks:
                 s_ps = psum.tile([P, BANK], F32, name="s_ps", tag="scores", bufs=BANKS)
                 nc.tensor.matmul(
                     out=s_ps[:],
@@ -157,19 +159,41 @@ def tile_spatialprocessor_pa_kernel(tc, q2, k2, v2, adj, x, proj_w, ln_g, ln_b, 
                 )
                 live["s_ps", t, b] = s_ps
 
-        def mask(t):
-            u = ring.tile([P, NODES], F32, name="u", tag="u")
-            for b in range(BANKS):
+        def mask(t, banks):
+            if ("u", t) not in live:
+                live["u", t] = ring.tile([P, NODES], F32, name="u", tag="u")
+            for b in banks:
                 cols = slice(BANK * b, BANK * (b + 1))
                 nc.vector.scalar_tensor_tensor(
-                    out=u[:, cols],
+                    out=live["u", t][:, cols],
                     in0=adj_sb[:, t, cols],
                     scalar=0.0,
                     in1=live["s_ps", t, b][:],
                     op0=ALU.is_equal,
                     op1=ALU.subtract,
                 )
-            live["u", t] = u
+
+        def has_away(t):
+            return 0 < t < TILES and t % 2 == 0
+
+        def no_edge(t):
+            flags = ring.tile([P, BANK], BF16, name="flags", tag="flags")
+            nc.vector.tensor_scalar(
+                out=flags[:],
+                in0=adj_sb[:, t, BANK * AWAY :],
+                scalar1=0.0,
+                scalar2=None,
+                op0=ALU.is_equal,
+            )
+            live["flags", t] = flags
+
+        def mask_away(t):
+            raw = ring.tile([P, BANK], F32, name="raw", tag="raw")
+            nc.scalar.copy(out=raw[:], in_=live["s_ps", t, AWAY][:])
+            live["u", t] = ring.tile([P, NODES], F32, name="u", tag="u")
+            nc.gpsimd.tensor_tensor(
+                out=live["u", t][:, BANK * AWAY :], in0=live["flags", t][:], in1=raw[:], op=ALU.subtract
+            )
 
         def row_min(t):
             u_min = stats.tile([P, 1], F32, name="u_min", tag="u_min")
@@ -359,16 +383,20 @@ def tile_spatialprocessor_pa_kernel(tc, q2, k2, v2, adj, x, proj_w, ln_g, ln_b, 
         transpose_queries(0)
         for b in range(1, BANKS):
             transpose_keys(b)
-        scores(0)
+        scores(0, range(BANKS))
         regroup_weights()
         last = TILES - 1
         for r in range(TILES):
-            mask(r)
+            mask(r, range(AWAY if has_away(r) else BANKS))
+            if has_away(r + 1):
+                no_edge(r + 1)
             if r < last:
-                scores(r + 1)
+                scores(r + 1, (AWAY, 0, 1, 2) if has_away(r + 1) else range(BANKS))
             transpose_x(r)
             if r >= 1:
                 exponentials(r - 1)
+            if has_away(r + 1):
+                mask_away(r + 1)
             if r >= 4 and r % 2 == 0:
                 out_of_psum((r - 4) // 2)
             if r >= 5 and r % 2 == 1:
@@ -413,8 +441,6 @@ def tile_spatialprocessor_pa_kernel(tc, q2, k2, v2, adj, x, proj_w, ln_g, ln_b, 
                 scale=-SCORE_SCALE,
                 accum_out=half_sum[:, h : h + 1],
             )
-        sum_squares(last // 2 - 1)
-        normalise(last // 2 - 1)
         e_words = e[:].bitcast(F32)
         e_grouped = ring.tile([P, PASSES, P, PACK], BF16, name="e_grouped", tag="e_grouped", align_bytes=64)
         e_codes = ring.tile([P, PASSES * P], U32, name="e_codes", tag="e_codes", align_bytes=64)
@@ -514,24 +540,26 @@ def tile_spatialprocessor_pa_kernel(tc, q2, k2, v2, adj, x, proj_w, ln_g, ln_b, 
         skip_out(last)
         last_regroup(0, nc.vector.tensor_copy)
         last_regroup(1, nc.vector.tensor_copy)
+        last_regroup(2, nc.scalar.copy)
+        sum_squares(last // 2 - 1)
+        normalise(last // 2 - 1)
         moments(t14)
+        inverse_deviation(t14)
         last_quantise(0, 2)
         attend_pass(last, 0)
         attend_pass(last, 1)
         row_sum = stats.tile([P, 1], F32, name="row_sum", tag="row_sum")
         nc.vector.tensor_tensor(out=row_sum[:], in0=half_sum[:, 0:1], in1=half_sum[:, 1:2], op=ALU.add)
-        last_regroup(3, nc.scalar.copy)
-        inverse_deviation(t14)
-        last_regroup(2, nc.vector.tensor_copy)
-        invert(last, row_sum[:])
-        centre(t14)
+        last_regroup(3, nc.vector.tensor_copy)
         last_quantise(2, 1)
+        invert(last, row_sum[:])
         last_quantise(3, 1)
         attend_pass(last, 2)
         attend_pass(last, 3)
-        finish(t14)
+        centre(t14)
         add_streams(last)
         moments(last)
         inverse_deviation(last)
         centre(last)
+        finish(t14)
         finish(last)

@@ -23,6 +23,7 @@ BANKS = NODES // BANK
 PACK = 4
 K_PASS = P * PACK
 PASSES = NODES // K_PASS
+TENSOR_MASKED = TILES - 1
 AWAY = BANKS - 1
 LN_EPS = 1e-3
 
@@ -68,17 +69,15 @@ def tile_spatialprocessor_pa_kernel(tc, q2, k2, v2, adj, x, proj_w, ln_g, ln_b, 
         def four(group):
             return slice(4 * group, 4 * group + 4)
 
-        half = NODES // 2
         nc.sync.dma_start(out=k_sb[:, 0, :], in_=k_rows[:, 0, :])
         nc.sync.dma_start(out=q_sb[:, four(0), :], in_=q_rows[:, four(0), :])
         for b in range(1, BANKS):
             nc.sync.dma_start(out=k_sb[:, b, :], in_=k_rows[:, b, :])
-        nc.sync.dma_start(out=adj_sb[:, 0, :half], in_=adj_rows[:, 0, :half])
-        nc.sync.dma_start(out=adj_sb[:, 0, half:], in_=adj_rows[:, 0, half:])
-        nc.sync.dma_start(out=v_sb[:], in_=v_rows)
-        nc.sync.dma_start(out=w_sb[:], in_=w_rows)
+        nc.sync.dma_start(out=adj_sb[:, 0, :], in_=adj_rows[:, 0, :])
         nc.sync.dma_start(out=adj_sb[:, 1, :], in_=adj_rows[:, 1, :])
         nc.sync.dma_start(out=x_sb[:, four(0), :], in_=x_rows[:, four(0), :])
+        nc.sync.dma_start(out=v_sb[:], in_=v_rows)
+        nc.sync.dma_start(out=w_sb[:], in_=w_rows)
         nc.sync.dma_start(out=q_sb[:, four(1), :], in_=q_rows[:, four(1), :])
         nc.sync.dma_start(out=adj_sb[:, 2, :], in_=adj_rows[:, 2, :])
         nc.sync.dma_start(out=adj_sb[:, 3, :], in_=adj_rows[:, 3, :])
@@ -99,21 +98,23 @@ def tile_spatialprocessor_pa_kernel(tc, q2, k2, v2, adj, x, proj_w, ln_g, ln_b, 
             kT_ps = psum.tile([D, 4, P], BF16, name="kT_ps", tag="scores", bufs=BANKS)
             for j in range(4):
                 nc.tensor.transpose(kT_ps[:, j, :], k_sb[:, b, D * j : D * (j + 1)], ident_bf[:])
-            nc.vector.tensor_scalar(
-                out=kT[:, BANK * b : BANK * (b + 1)].rearrange("d (p j) -> d p j", j=4),
-                in0=kT_ps[:].rearrange("d j p -> d p j"),
-                scalar1=K_SHRINK,
-                scalar2=None,
-                op0=ALU.mult,
-            )
+            natural = kT[:, BANK * b : BANK * (b + 1)].rearrange("d (p j) -> d p j", j=4)
+            in_ = kT_ps[:].rearrange("d j p -> d p j")
+            if b % 2 == 0:
+                nc.vector.tensor_scalar(out=natural, in0=in_, scalar1=K_SHRINK, scalar2=None, op0=ALU.mult)
+            else:
+                nc.scalar.mul(out=natural, in_=in_, mul=K_SHRINK)
 
         def transpose_queries(group):
             qT_ps = psum.tile([D, 4, P], BF16, name="qT_ps", tag="eT", bufs=2)
             for c in range(4):
                 nc.tensor.transpose(qT_ps[:, c, :], q_sb[:, 4 * group + c, :], ident_bf[:])
-            cuts = (0, 1, 4) if group == 0 else (0, 4)
-            for lo, hi in zip(cuts[:-1], cuts[1:]):
-                nc.scalar.copy(out=qT[:, 4 * group + lo : 4 * group + hi, :], in_=qT_ps[:, lo:hi, :])
+            live["qT_ps", group] = qT_ps
+
+        def queries_out(group, lo, hi):
+            nc.scalar.copy(
+                out=qT[:, 4 * group + lo : 4 * group + hi, :], in_=live["qT_ps", group][:, lo:hi, :]
+            )
 
         v_grouped = keep.tile([P, PASSES, D, PACK], BF16, name="v_grouped", align_bytes=64)
         v_codes = keep.tile([P, PASSES * D], U32, name="v_codes", align_bytes=64)
@@ -124,13 +125,21 @@ def tile_spatialprocessor_pa_kernel(tc, q2, k2, v2, adj, x, proj_w, ln_g, ln_b, 
 
         def regroup_weights():
             for g in range(PASSES):
-                nc.scalar.copy(
+                nc.gpsimd.tensor_scalar(
                     out=v_grouped[:, g, :, :].rearrange("p d (u e) -> p d u e", e=2),
-                    in_=v_sb[:, 2 * g : 2 * g + 2, :].rearrange("p u (e d) -> p d u e", e=2),
+                    in0=v_sb[:, 2 * g : 2 * g + 2, :].rearrange("p u (e d) -> p d u e", e=2),
+                    scalar1=1.0,
+                    scalar2=0.0,
+                    op0=ALU.mult,
+                    op1=ALU.add,
                 )
-            nc.scalar.copy(
+            nc.gpsimd.tensor_scalar(
                 out=w_grouped[:].rearrange("p d (u e) -> p d u e", e=2),
-                in_=w_sb[:].rearrange("p u (e d) -> p d u e", e=2),
+                in0=w_sb[:].rearrange("p u (e d) -> p d u e", e=2),
+                scalar1=1.0,
+                scalar2=0.0,
+                op0=ALU.mult,
+                op1=ALU.add,
             )
 
         def quantise_weights():
@@ -173,8 +182,58 @@ def tile_spatialprocessor_pa_kernel(tc, q2, k2, v2, adj, x, proj_w, ln_g, ln_b, 
                     op1=ALU.subtract,
                 )
 
+        def row_sum(t):
+            if ("row_sums", t // 2) not in live:
+                live["row_sums", t // 2] = stats.tile([P, 2], F32, name="row_sums", tag="row_sums")
+            return live["row_sums", t // 2][:, t % 2 : t % 2 + 1]
+
         def has_away(t):
-            return 0 < t < TILES and t % 2 == 0
+            return 0 < t < TILES and t % 2 == 0 and t != TENSOR_MASKED
+
+        def minus_no_edge(t):
+            minus = ring.tile([P, NODES], BF16, name="minus", tag="minus", bufs=2)
+            nc.vector.tensor_scalar(
+                out=minus[:], in0=adj_sb[:, t, :], scalar1=0.0, scalar2=-1.0, op0=ALU.is_equal, op1=ALU.mult
+            )
+            live["minus", t] = minus
+
+        def masked_scores(t):
+            for b in range(BANKS):
+                cols = slice(BANK * b, BANK * (b + 1))
+                s_ps = psum.tile([P, BANK], F32, name="s_ps", tag="scores", bufs=BANKS)
+                nc.tensor.matmul(out=s_ps[:], lhsT=qT[:, t, :], rhs=kT[:, cols], start=True, stop=False)
+                nc.tensor.matmul(out=s_ps[:], lhsT=ident_bf[:], rhs=live["minus", t][:, cols], start=False, stop=True)
+                live["s_ps", t, b] = s_ps
+
+        def row_max(t):
+            bank_max = stats.tile([P, BANKS], F32, name="bank_max", tag="bank_max")
+            for b in range(BANKS):
+                nc.vector.tensor_reduce(
+                    out=bank_max[:, b : b + 1], in_=live["s_ps", t, b][:], axis=AXIS.X, op=ALU.max
+                )
+            u_max = stats.tile([P, 1], F32, name="u_max", tag="u_max")
+            nc.vector.tensor_reduce(out=u_max[:], in_=bank_max[:], axis=AXIS.X, op=ALU.max)
+            live["u_max", t] = u_max
+
+        def exponentials_from_psum(t):
+            minus_max = stats.tile([P, 1], F32, name="minus_max", tag="minus_max")
+            nc.scalar.mul(out=minus_max[:], in_=live["u_max", t][:], mul=-SCORE_SCALE)
+            e = ring.tile([P, NODES], BF16, name="e", tag="e")
+            bank_sums = stats.tile([P, BANKS], F32, name="bank_sums", tag="bank_sums")
+            for b in range(BANKS):
+                nc.scalar.activation(
+                    out=e[:, BANK * b : BANK * (b + 1)],
+                    in_=live["s_ps", t, b][:],
+                    func=ACT.Exp,
+                    bias=minus_max[:, 0:1],
+                    scale=SCORE_SCALE,
+                    accum_out=bank_sums[:, b : b + 1],
+                )
+            live["e", t] = e
+            live["bank_sums", t] = bank_sums
+
+        def total(t):
+            nc.vector.tensor_reduce(out=row_sum(t), in_=live["bank_sums", t][:], axis=AXIS.X, op=ALU.add)
 
         def no_edge(t):
             flags = ring.tile([P, BANK], BF16, name="flags", tag="flags")
@@ -204,16 +263,13 @@ def tile_spatialprocessor_pa_kernel(tc, q2, k2, v2, adj, x, proj_w, ln_g, ln_b, 
             max_score = stats.tile([P, 1], F32, name="max_score", tag="max_score")
             nc.scalar.mul(out=max_score[:], in_=live["u_min", t][:], mul=SCORE_SCALE)
             e = ring.tile([P, NODES], BF16, name="e", tag="e")
-            if t % 2 == 0:
-                live["row_sums", t // 2] = stats.tile([P, 2], F32, name="row_sums", tag="row_sums")
-            row_sum = live["row_sums", t // 2][:, t % 2 : t % 2 + 1]
             nc.scalar.activation(
                 out=e[:],
                 in_=live["u", t][:],
                 func=ACT.Exp,
                 bias=max_score[:, 0:1],
                 scale=-SCORE_SCALE,
-                accum_out=row_sum,
+                accum_out=row_sum(t),
             )
             live["e", t] = e
 
@@ -242,9 +298,9 @@ def tile_spatialprocessor_pa_kernel(tc, q2, k2, v2, adj, x, proj_w, ln_g, ln_b, 
                 )
             live["e_grouped", t] = e_grouped
 
-        def regroup_x(t):
+        def regroup_x(t, copy):
             x_grouped = ring.tile([P, P, PACK], BF16, name="x_grouped", tag="x_grouped", align_bytes=64)
-            nc.scalar.copy(out=x_grouped[:].bitcast(F32), in_=live["xT_ps", t][:].rearrange("p u q -> p q u"))
+            copy(out=x_grouped[:].bitcast(F32), in_=live["xT_ps", t][:].rearrange("p u q -> p q u"))
             live["x_grouped", t] = x_grouped
 
         def quantise_e(t):
@@ -356,6 +412,10 @@ def tile_spatialprocessor_pa_kernel(tc, q2, k2, v2, adj, x, proj_w, ln_g, ln_b, 
                 op0=ALU.mult,
                 op1=ALU.add,
             )
+            means = [live["neg_means", pair][:, i : i + 1] for i in range(2)]
+            scale_and_store(pair, vars_eps, means, ALU.add)
+
+        def scale_and_store(pair, vars_eps, means, centre_op):
             inv_stds = stats.tile([P, 2], F32, name="inv_stds", tag="inv_stds")
             nc.gpsimd.tensor_tensor(out=inv_stds[:], in0=vars_eps[:], in1=neg_half[:], op=ALU.pow)
             normed = ring.tile([P, 2, D], F32, name="normed", tag="normed")
@@ -363,9 +423,9 @@ def tile_spatialprocessor_pa_kernel(tc, q2, k2, v2, adj, x, proj_w, ln_g, ln_b, 
                 nc.gpsimd.tensor_scalar(
                     out=normed[:, i, :],
                     in0=live["y", pair][:, i, :],
-                    scalar1=live["neg_means", pair][:, i : i + 1],
+                    scalar1=means[i],
                     scalar2=inv_stds[:, i : i + 1],
-                    op0=ALU.add,
+                    op0=centre_op,
                     op1=ALU.mult,
                 )
             scaled = ring.tile([P, 2, D], F32, name="scaled", tag="scaled")
@@ -381,18 +441,26 @@ def tile_spatialprocessor_pa_kernel(tc, q2, k2, v2, adj, x, proj_w, ln_g, ln_b, 
         stack.enter_context(tc.manual_schedule())
         transpose_keys(0)
         transpose_queries(0)
+        queries_out(0, 0, 1)
         for b in range(1, BANKS):
             transpose_keys(b)
+        queries_out(0, 1, 4)
         scores(0, range(BANKS))
         regroup_weights()
         last = TILES - 1
         for r in range(TILES):
-            mask(r, range(AWAY if has_away(r) else BANKS))
+            if r != TENSOR_MASKED:
+                mask(r, range(AWAY if has_away(r) else BANKS))
+            if r + 2 == last:
+                minus_no_edge(last)
             if has_away(r + 1):
                 no_edge(r + 1)
-            if r < last:
+            if r + 1 == last:
+                masked_scores(last)
+            elif r < last:
                 scores(r + 1, (AWAY, 0, 1, 2) if has_away(r + 1) else range(BANKS))
-            transpose_x(r)
+            if r < last:
+                transpose_x(r)
             if r >= 1:
                 exponentials(r - 1)
             if has_away(r + 1):
@@ -402,13 +470,15 @@ def tile_spatialprocessor_pa_kernel(tc, q2, k2, v2, adj, x, proj_w, ln_g, ln_b, 
             if r >= 5 and r % 2 == 1:
                 sum_squares((r - 5) // 2)
                 normalise((r - 5) // 2)
-            regroup_x(r)
+            if r < last - 1:
+                regroup_x(r, nc.scalar.copy)
             if r in (2, 6, 10):
                 transpose_queries((r + 2) // 4)
-            if r >= 1:
+                queries_out((r + 2) // 4, 0, 4)
+            if 1 <= r < last:
                 transpose_e(r - 1)
                 regroup_e(r - 1)
-            if r == 1:
+            if r == 2:
                 quantise_weights()
             if r >= 3 and r % 2 == 1:
                 invert_sums((r - 3) // 2)
@@ -417,35 +487,61 @@ def tile_spatialprocessor_pa_kernel(tc, q2, k2, v2, adj, x, proj_w, ln_g, ln_b, 
                 quantise_x(r - 2)
                 attend(r - 2)
             if r == last:
-                out_of_psum((r - 3) // 2)
-            row_min(r)
+                transpose_e(last - 1)
+                regroup_e(last - 1)
+                regroup_x(last - 1, nc.vector.tensor_copy)
+                transpose_x(last)
+                quantise_x(last - 1)
+            if r == TENSOR_MASKED:
+                row_max(r)
+            else:
+                row_min(r)
+
+        def last_pair_streams(pair):
+            acc = live["acc", pair]
+            skip = ring.tile([P, 2, D], F32, name="skip", tag="skip")
+            nc.vector.tensor_copy(out=skip[:], in_=acc[:, :, 1, :])
+            y = ring.tile([P, 2, D], F32, name="y", tag="y")
+            for i in range(2):
+                nc.vector.scalar_tensor_tensor(
+                    out=y[:, i, :],
+                    in0=acc[:, i, 0, :],
+                    scalar=live["inv_sums", pair][:, i : i + 1],
+                    in1=skip[:, i, :],
+                    op0=ALU.mult,
+                    op1=ALU.add,
+                )
+            parts = stats.tile([P, 2, 6], F32, name="parts", tag="parts")
+            for i in range(2):
+                nc.vector.bn_stats(out=parts[:, i, :], in_=y[:, i, :])
+            mean_vars = stats.tile([P, 2, 2], F32, name="mean_vars", tag="mean_vars")
+            for i in range(2):
+                nc.vector.bn_aggr(out=mean_vars[:, i, :], in_=parts[:, i, :])
+            live["y", pair] = y
+            live["mean_vars", pair] = mean_vars
 
         t14 = last - 1
+        last_pair_streams(t14 // 2 - 1)
         quantise_e(t14)
-        quantise_x(t14)
+        regroup_x(last, nc.vector.tensor_copy)
         quantise_x(last)
         attend(t14)
         project(last)
 
-        max_score = stats.tile([P, 1], F32, name="max_score", tag="max_score")
-        nc.scalar.mul(out=max_score[:], in_=live["u_min", last][:], mul=SCORE_SCALE)
-        e = ring.tile([P, NODES], BF16, name="e", tag="e")
-        half_sum = stats.tile([P, 2], F32, name="half_sum", tag="half_sum")
-        for h in range(2):
-            cols = slice(NODES // 2 * h, NODES // 2 * (h + 1))
-            nc.scalar.activation(
-                out=e[:, cols],
-                in_=live["u", last][:, cols],
-                func=ACT.Exp,
-                bias=max_score[:, 0:1],
-                scale=-SCORE_SCALE,
-                accum_out=half_sum[:, h : h + 1],
-            )
-        e_words = e[:].bitcast(F32)
+        exponentials_from_psum(last)
+        e_words = live["e", last][:].bitcast(F32)
         e_grouped = ring.tile([P, PASSES, P, PACK], BF16, name="e_grouped", tag="e_grouped", align_bytes=64)
         e_codes = ring.tile([P, PASSES * P], U32, name="e_codes", tag="e_codes", align_bytes=64)
         e_scales = ring.tile([P, PASSES * P], U8, name="e_scales", tag="e_scales", align_bytes=64)
         live["e_mx", last] = (e_codes, e_scales)
+
+        def normalise_last_pair(pair):
+            mean_vars = live["mean_vars", pair]
+            vars_eps = stats.tile([P, 2], F32, name="vars_eps", tag="vars_eps")
+            nc.gpsimd.tensor_scalar(
+                out=vars_eps[:], in0=mean_vars[:, :, 1], scalar1=1.0, scalar2=LN_EPS, op0=ALU.mult, op1=ALU.add
+            )
+            scale_and_store(pair, vars_eps, [mean_vars[:, i, 0:1] for i in range(2)], ALU.subtract)
 
         def last_transposes(g):
             eT_ps = psum.tile([P, 2, P], F32, name="eT_last", tag="scores", bufs=BANKS)
@@ -473,9 +569,9 @@ def tile_spatialprocessor_pa_kernel(tc, q2, k2, v2, adj, x, proj_w, ln_g, ln_b, 
             nc.vector.tensor_copy(out=skip[:], in_=live["acc", t // 2][:, t % 2, 1, :])
             live["skip", t] = skip
 
-        def invert(t, row_sum):
+        def invert(t):
             inv_sum = stats.tile([P, 1], F32, name="inv_sum", tag="inv_sum")
-            nc.vector.reciprocal(out=inv_sum[:], in_=row_sum)
+            nc.vector.reciprocal(out=inv_sum[:], in_=row_sum(t))
             live["inv_sum", t] = inv_sum
 
         def add_streams(t):
@@ -534,25 +630,23 @@ def tile_spatialprocessor_pa_kernel(tc, q2, k2, v2, adj, x, proj_w, ln_g, ln_b, 
 
         for g in range(PASSES):
             last_transposes(g)
-        invert(t14, live["row_sums", t14 // 2][:, 0:1])
         skip_out(t14)
+        invert(t14)
         add_streams(t14)
         skip_out(last)
         last_regroup(0, nc.vector.tensor_copy)
         last_regroup(1, nc.vector.tensor_copy)
         last_regroup(2, nc.scalar.copy)
-        sum_squares(last // 2 - 1)
-        normalise(last // 2 - 1)
+        normalise_last_pair(t14 // 2 - 1)
         moments(t14)
         inverse_deviation(t14)
         last_quantise(0, 2)
         attend_pass(last, 0)
         attend_pass(last, 1)
-        row_sum = stats.tile([P, 1], F32, name="row_sum", tag="row_sum")
-        nc.vector.tensor_tensor(out=row_sum[:], in0=half_sum[:, 0:1], in1=half_sum[:, 1:2], op=ALU.add)
+        total(last)
         last_regroup(3, nc.vector.tensor_copy)
         last_quantise(2, 1)
-        invert(last, row_sum[:])
+        invert(last)
         last_quantise(3, 1)
         attend_pass(last, 2)
         attend_pass(last, 3)

@@ -24,7 +24,6 @@ PACK = 4
 K_PASS = P * PACK
 PASSES = NODES // K_PASS
 TENSOR_MASKED = TILES - 1
-AWAY = BANKS - 1
 LN_EPS = 1e-3
 
 K_SHRINK = 2.0 ** -34
@@ -187,8 +186,15 @@ def tile_spatialprocessor_pa_kernel(tc, q2, k2, v2, adj, x, proj_w, ln_g, ln_b, 
                 live["row_sums", t // 2] = stats.tile([P, 2], F32, name="row_sums", tag="row_sums")
             return live["row_sums", t // 2][:, t % 2 : t % 2 + 1]
 
-        def has_away(t):
-            return 0 < t < TILES and t % 2 == 0 and t != TENSOR_MASKED
+        def away(t):
+            if t in (0, TENSOR_MASKED):
+                return ()
+            if t == 1:
+                return (2, 3)
+            return (3,) if t % 2 == 0 or t == 3 else ()
+
+        def kept(t):
+            return tuple(b for b in range(BANKS) if b not in away(t))
 
         def minus_no_edge(t):
             minus = ring.tile([P, NODES], BF16, name="minus", tag="minus", bufs=2)
@@ -236,10 +242,11 @@ def tile_spatialprocessor_pa_kernel(tc, q2, k2, v2, adj, x, proj_w, ln_g, ln_b, 
             nc.vector.tensor_reduce(out=row_sum(t), in_=live["bank_sums", t][:], axis=AXIS.X, op=ALU.add)
 
         def no_edge(t):
-            flags = ring.tile([P, BANK], BF16, name="flags", tag="flags")
+            first = away(t)[0]
+            flags = ring.tile([P, BANKS * BANK // 2], BF16, name="flags", tag="flags")
             nc.vector.tensor_scalar(
-                out=flags[:],
-                in0=adj_sb[:, t, BANK * AWAY :],
+                out=flags[:, : NODES - BANK * first],
+                in0=adj_sb[:, t, BANK * first :],
                 scalar1=0.0,
                 scalar2=None,
                 op0=ALU.is_equal,
@@ -247,12 +254,17 @@ def tile_spatialprocessor_pa_kernel(tc, q2, k2, v2, adj, x, proj_w, ln_g, ln_b, 
             live["flags", t] = flags
 
         def mask_away(t):
-            raw = ring.tile([P, BANK], F32, name="raw", tag="raw")
-            nc.scalar.copy(out=raw[:], in_=live["s_ps", t, AWAY][:])
-            live["u", t] = ring.tile([P, NODES], F32, name="u", tag="u")
-            nc.gpsimd.tensor_tensor(
-                out=live["u", t][:, BANK * AWAY :], in0=live["flags", t][:], in1=raw[:], op=ALU.subtract
-            )
+            if ("u", t) not in live:
+                live["u", t] = ring.tile([P, NODES], F32, name="u", tag="u")
+            for i, b in reversed(tuple(enumerate(away(t)))):
+                raw = ring.tile([P, BANK], F32, name="raw", tag="raw")
+                nc.scalar.copy(out=raw[:], in_=live["s_ps", t, b][:])
+                nc.gpsimd.tensor_tensor(
+                    out=live["u", t][:, BANK * b : BANK * (b + 1)],
+                    in0=live["flags", t][:, BANK * i : BANK * (i + 1)],
+                    in1=raw[:],
+                    op=ALU.subtract,
+                )
 
         def row_min(t):
             u_min = stats.tile([P, 1], F32, name="u_min", tag="u_min")
@@ -445,26 +457,27 @@ def tile_spatialprocessor_pa_kernel(tc, q2, k2, v2, adj, x, proj_w, ln_g, ln_b, 
         for b in range(1, BANKS):
             transpose_keys(b)
         queries_out(0, 1, 4)
-        scores(0, range(BANKS))
-        regroup_weights()
+        scores(0, kept(0))
         last = TILES - 1
         for r in range(TILES):
             if r != TENSOR_MASKED:
-                mask(r, range(AWAY if has_away(r) else BANKS))
+                mask(r, kept(r))
             if r + 2 == last:
                 minus_no_edge(last)
-            if has_away(r + 1):
+            if r < last and away(r + 1):
                 no_edge(r + 1)
             if r + 1 == last:
                 masked_scores(last)
             elif r < last:
-                scores(r + 1, (AWAY, 0, 1, 2) if has_away(r + 1) else range(BANKS))
+                scores(r + 1, away(r + 1)[::-1] + kept(r + 1))
             if r < last:
                 transpose_x(r)
             if r >= 1:
                 exponentials(r - 1)
-            if has_away(r + 1):
+            if r < last:
                 mask_away(r + 1)
+            if r == 0:
+                regroup_weights()
             if r >= 4 and r % 2 == 0:
                 out_of_psum((r - 4) // 2)
             if r >= 5 and r % 2 == 1:
@@ -497,7 +510,7 @@ def tile_spatialprocessor_pa_kernel(tc, q2, k2, v2, adj, x, proj_w, ln_g, ln_b, 
             else:
                 row_min(r)
 
-        def last_pair_streams(pair):
+        def pair_streams(pair):
             acc = live["acc", pair]
             skip = ring.tile([P, 2, D], F32, name="skip", tag="skip")
             nc.vector.tensor_copy(out=skip[:], in_=acc[:, :, 1, :])
@@ -511,20 +524,23 @@ def tile_spatialprocessor_pa_kernel(tc, q2, k2, v2, adj, x, proj_w, ln_g, ln_b, 
                     op0=ALU.mult,
                     op1=ALU.add,
                 )
+            live["y", pair] = y
+
+        def pair_moments(pair):
             parts = stats.tile([P, 2, 6], F32, name="parts", tag="parts")
             for i in range(2):
-                nc.vector.bn_stats(out=parts[:, i, :], in_=y[:, i, :])
+                nc.vector.bn_stats(out=parts[:, i, :], in_=live["y", pair][:, i, :])
             mean_vars = stats.tile([P, 2, 2], F32, name="mean_vars", tag="mean_vars")
             for i in range(2):
                 nc.vector.bn_aggr(out=mean_vars[:, i, :], in_=parts[:, i, :])
-            live["y", pair] = y
             live["mean_vars", pair] = mean_vars
 
         t14 = last - 1
-        last_pair_streams(t14 // 2 - 1)
+        pair_streams(t14 // 2 - 1)
         quantise_e(t14)
         regroup_x(last, nc.vector.tensor_copy)
         quantise_x(last)
+        pair_moments(t14 // 2 - 1)
         attend(t14)
         project(last)
 
@@ -544,7 +560,10 @@ def tile_spatialprocessor_pa_kernel(tc, q2, k2, v2, adj, x, proj_w, ln_g, ln_b, 
             scale_and_store(pair, vars_eps, [mean_vars[:, i, 0:1] for i in range(2)], ALU.subtract)
 
         def last_transposes(g):
-            eT_ps = psum.tile([P, 2, P], F32, name="eT_last", tag="scores", bufs=BANKS)
+            if g < 2:
+                eT_ps = psum.tile([P, 2, P], F32, name="eT_last", tag="eT", bufs=2)
+            else:
+                eT_ps = psum.tile([P, 2, P], F32, name="eT_last", tag="scores", bufs=BANKS)
             for u in range(2):
                 chunk = 2 * g + u
                 nc.tensor.transpose(eT_ps[:, u, :], e_words[:, P * chunk : P * (chunk + 1)], ident_f32[:])
@@ -564,10 +583,10 @@ def tile_spatialprocessor_pa_kernel(tc, q2, k2, v2, adj, x, proj_w, ln_g, ln_b, 
                 in_=e_grouped[:, g : g + passes, :, :].rearrange("p g q j -> p (g q j)"),
             )
 
-        def skip_out(t):
-            skip = ring.tile([P, D], F32, name="skip", tag="skip")
-            nc.vector.tensor_copy(out=skip[:], in_=live["acc", t // 2][:, t % 2, 1, :])
-            live["skip", t] = skip
+        def last_skips():
+            skips = ring.tile([P, 2, D], F32, name="skip", tag="skip")
+            nc.vector.tensor_copy(out=skips[:], in_=live["acc", last // 2][:, :, 1, :])
+            live["skips"] = skips
 
         def invert(t):
             inv_sum = stats.tile([P, 1], F32, name="inv_sum", tag="inv_sum")
@@ -580,7 +599,7 @@ def tile_spatialprocessor_pa_kernel(tc, q2, k2, v2, adj, x, proj_w, ln_g, ln_b, 
                 out=y[:],
                 in0=live["acc", t // 2][:, t % 2, 0, :],
                 scalar=live["inv_sum", t][:, 0:1],
-                in1=live["skip", t][:],
+                in1=live["skips"][:, t % 2, :],
                 op0=ALU.mult,
                 op1=ALU.add,
             )
@@ -628,18 +647,15 @@ def tile_spatialprocessor_pa_kernel(tc, q2, k2, v2, adj, x, proj_w, ln_g, ln_b, 
             )
             nc.sync.dma_start(out=out_rows[:, t, :], in_=result[:])
 
+        normalise_last_pair(t14 // 2 - 1)
         for g in range(PASSES):
             last_transposes(g)
-        skip_out(t14)
         invert(t14)
-        add_streams(t14)
-        skip_out(last)
+        last_skips()
         last_regroup(0, nc.vector.tensor_copy)
+        add_streams(t14)
         last_regroup(1, nc.vector.tensor_copy)
         last_regroup(2, nc.scalar.copy)
-        normalise_last_pair(t14 // 2 - 1)
-        moments(t14)
-        inverse_deviation(t14)
         last_quantise(0, 2)
         attend_pass(last, 0)
         attend_pass(last, 1)
@@ -650,10 +666,12 @@ def tile_spatialprocessor_pa_kernel(tc, q2, k2, v2, adj, x, proj_w, ln_g, ln_b, 
         last_quantise(3, 1)
         attend_pass(last, 2)
         attend_pass(last, 3)
-        centre(t14)
+        moments(t14)
+        inverse_deviation(t14)
         add_streams(last)
+        centre(t14)
         moments(last)
         inverse_deviation(last)
-        centre(last)
         finish(t14)
+        centre(last)
         finish(last)

import math
from contextlib import ExitStack

import concourse.mybir as mybir
from concourse.masks import make_identity

F32 = mybir.dt.float32
BF16 = mybir.dt.bfloat16
U32 = mybir.dt.uint32
U8 = mybir.dt.uint8
FP8X4 = mybir.dt.float8_e4m3fn_x4
ALU = mybir.AluOpType
ACT = mybir.ActivationFunctionType
AXIS = mybir.AxisListType

P = 128
NODES = 2048
D = 128
F_IN = 512
TILES = NODES // P
BANK = 512
BANKS = NODES // BANK
PACK = 4
K_PASS = P * PACK
PASSES = NODES // K_PASS
TENSOR_MASKED = TILES - 1
LN_EPS = 1e-3

K_SHRINK = 2.0 ** -34
SCORE_SCALE = 2.0 ** 34 / math.sqrt(D)

FLOPS = 2 * NODES * NODES * D * 2 + 2 * NODES * F_IN * D


def tile_spatialprocessor_pa_kernel(tc, q2, k2, v2, adj, x, proj_w, ln_g, ln_b, out):
    nc = tc.nc

    q_rows = q2.flatten_outer_dims().rearrange("(p t) d -> p t d", t=TILES)
    adj_rows = adj.rearrange("(p t) k -> p t k", t=TILES)
    x_rows = x.flatten_outer_dims().rearrange("(p t) f -> p t f", t=TILES)
    out_rows = out.flatten_outer_dims().rearrange("(p t) d -> p t d", t=TILES)
    k_rows = k2.flatten_outer_dims().rearrange("(b p j) d -> p b (j d)", p=P, j=4)
    v_rows = v2.flatten_outer_dims().rearrange("(c p e) d -> p c (e d)", p=P, e=2)
    w_rows = proj_w.rearrange("(u p e) d -> p u (e d)", u=2, e=2)

    with ExitStack() as stack:
        keep = stack.enter_context(tc.tile_pool(name="keep", bufs=1))
        ring = stack.enter_context(tc.tile_pool(name="ring", bufs=3))
        stats = stack.enter_context(tc.tile_pool(name="stats", bufs=6))
        psum = stack.enter_context(tc.psum_pool(name="psum", bufs=1))

        ident_bf = keep.tile([P, P], BF16, name="ident_bf")
        make_identity(nc, ident_bf[:])
        ident_f32 = keep.tile([P, P], F32, name="ident_f32")
        make_identity(nc, ident_f32[:])
        neg_half = keep.tile([P, 2], F32, name="neg_half")
        nc.gpsimd.memset(neg_half[:], -0.5)

        k_sb = keep.tile([P, BANKS, 4 * D], BF16, name="k_sb")
        q_sb = keep.tile([P, TILES, D], BF16, name="q_sb")
        v_sb = keep.tile([P, TILES // 2, 2 * D], BF16, name="v_sb")
        w_sb = keep.tile([P, 2, 2 * D], BF16, name="w_sb")
        x_sb = keep.tile([P, TILES, F_IN], BF16, name="x_sb")
        adj_sb = keep.tile([P, TILES, NODES], BF16, name="adj_sb")
        gain = keep.tile([P, D], BF16, name="gain")
        shift = keep.tile([P, D], BF16, name="shift")

        def four(group):
            return slice(4 * group, 4 * group + 4)

        nc.sync.dma_start(out=k_sb[:, 0, :], in_=k_rows[:, 0, :])
        nc.sync.dma_start(out=q_sb[:, four(0), :], in_=q_rows[:, four(0), :])
        for b in range(1, BANKS):
            nc.sync.dma_start(out=k_sb[:, b, :], in_=k_rows[:, b, :])
        nc.sync.dma_start(out=adj_sb[:, 0, :], in_=adj_rows[:, 0, :])
        nc.sync.dma_start(out=adj_sb[:, 1, :], in_=adj_rows[:, 1, :])
        nc.sync.dma_start(out=x_sb[:, four(0), :], in_=x_rows[:, four(0), :])
        nc.sync.dma_start(out=v_sb[:], in_=v_rows)
        nc.sync.dma_start(out=w_sb[:], in_=w_rows)
        nc.sync.dma_start(out=q_sb[:, four(1), :], in_=q_rows[:, four(1), :])
        nc.sync.dma_start(out=adj_sb[:, 2, :], in_=adj_rows[:, 2, :])
        nc.sync.dma_start(out=adj_sb[:, 3, :], in_=adj_rows[:, 3, :])
        for group in range(1, 4):
            nc.sync.dma_start(out=x_sb[:, four(group), :], in_=x_rows[:, four(group), :])
            if group > 1:
                nc.sync.dma_start(out=q_sb[:, four(group), :], in_=q_rows[:, four(group), :])
            for t in range(4 * group, 4 * group + 4):
                nc.sync.dma_start(out=adj_sb[:, t, :], in_=adj_rows[:, t, :])
            if group == 1:
                nc.sync.dma_start(out=gain[:], in_=ln_g.partition_broadcast(P))
                nc.sync.dma_start(out=shift[:], in_=ln_b.partition_broadcast(P))

        kT = keep.tile([D, NODES], BF16, name="kT")
        qT = keep.tile([D, TILES, P], BF16, name="qT")

        def transpose_keys(b):
            kT_ps = psum.tile([D, 4, P], BF16, name="kT_ps", tag="scores", bufs=BANKS)
            for j in range(4):
                nc.tensor.transpose(kT_ps[:, j, :], k_sb[:, b, D * j : D * (j + 1)], ident_bf[:])
            natural = kT[:, BANK * b : BANK * (b + 1)].rearrange("d (p j) -> d p j", j=4)
            in_ = kT_ps[:].rearrange("d j p -> d p j")
            if b % 2 == 0:
                nc.vector.tensor_scalar(out=natural, in0=in_, scalar1=K_SHRINK, scalar2=None, op0=ALU.mult)
            else:
                nc.scalar.mul(out=natural, in_=in_, mul=K_SHRINK)

        def transpose_queries(group):
            qT_ps = psum.tile([D, 4, P], BF16, name="qT_ps", tag="eT", bufs=2)
            for c in range(4):
                nc.tensor.transpose(qT_ps[:, c, :], q_sb[:, 4 * group + c, :], ident_bf[:])
            live["qT_ps", group] = qT_ps

        def queries_out(group, lo, hi):
            nc.scalar.copy(
                out=qT[:, 4 * group + lo : 4 * group + hi, :], in_=live["qT_ps", group][:, lo:hi, :]
            )

        v_grouped = keep.tile([P, PASSES, D, PACK], BF16, name="v_grouped", align_bytes=64)
        v_codes = keep.tile([P, PASSES * D], U32, name="v_codes", align_bytes=64)
        v_scales = keep.tile([P, PASSES * D], U8, name="v_scales", align_bytes=64)
        w_grouped = keep.tile([P, D, PACK], BF16, name="w_grouped", align_bytes=64)
        w_codes = keep.tile([P, D], U32, name="w_codes", align_bytes=64)
        w_scales = keep.tile([P, D], U8, name="w_scales", align_bytes=64)

        def regroup_weights():
            for g in range(PASSES):
                nc.gpsimd.tensor_scalar(
                    out=v_grouped[:, g, :, :].rearrange("p d (u e) -> p d u e", e=2),
                    in0=v_sb[:, 2 * g : 2 * g + 2, :].rearrange("p u (e d) -> p d u e", e=2),
                    scalar1=1.0,
                    scalar2=0.0,
                    op0=ALU.mult,
                    op1=ALU.add,
                )
            nc.gpsimd.tensor_scalar(
                out=w_grouped[:].rearrange("p d (u e) -> p d u e", e=2),
                in0=w_sb[:].rearrange("p u (e d) -> p d u e", e=2),
                scalar1=1.0,
                scalar2=0.0,
                op0=ALU.mult,
                op1=ALU.add,
            )

        def quantise_weights():
            nc.vector.quantize_mx(
                out=v_codes[:].bitcast(FP8X4),
                scales=v_scales[:],
                in_=v_grouped[:].rearrange("p g d j -> p (g d j)"),
            )
            nc.vector.quantize_mx(
                out=w_codes[:].bitcast(FP8X4),
                scales=w_scales[:],
                in_=w_grouped[:].rearrange("p d j -> p (d j)"),
            )

        live = {}

        def scores(t, banks):
            for b in banks:
                s_ps = psum.tile([P, BANK], F32, name="s_ps", tag="scores", bufs=BANKS)
                nc.tensor.matmul(
                    out=s_ps[:],
                    lhsT=qT[:, t, :],
                    rhs=kT[:, BANK * b : BANK * (b + 1)],
                    start=True,
                    stop=True,
                )
                live["s_ps", t, b] = s_ps

        def mask(t, banks):
            if ("u", t) not in live:
                live["u", t] = ring.tile([P, NODES], F32, name="u", tag="u")
            for b in banks:
                cols = slice(BANK * b, BANK * (b + 1))
                nc.vector.scalar_tensor_tensor(
                    out=live["u", t][:, cols],
                    in0=adj_sb[:, t, cols],
                    scalar=0.0,
                    in1=live["s_ps", t, b][:],
                    op0=ALU.is_equal,
                    op1=ALU.subtract,
                )

        def row_sum(t):
            if ("row_sums", t // 2) not in live:
                live["row_sums", t // 2] = stats.tile([P, 2], F32, name="row_sums", tag="row_sums")
            return live["row_sums", t // 2][:, t % 2 : t % 2 + 1]

        def away(t):
            if t in (0, TENSOR_MASKED):
                return ()
            if t == 1:
                return (2, 3)
            return (3,) if t % 2 == 0 or t == 3 else ()

        def kept(t):
            return tuple(b for b in range(BANKS) if b not in away(t))

        def minus_no_edge(t):
            minus = ring.tile([P, NODES], BF16, name="minus", tag="minus", bufs=2)
            nc.vector.tensor_scalar(
                out=minus[:], in0=adj_sb[:, t, :], scalar1=0.0, scalar2=-1.0, op0=ALU.is_equal, op1=ALU.mult
            )
            live["minus", t] = minus

        def masked_scores(t):
            for b in range(BANKS):
                cols = slice(BANK * b, BANK * (b + 1))
                s_ps = psum.tile([P, BANK], F32, name="s_ps", tag="scores", bufs=BANKS)
                nc.tensor.matmul(out=s_ps[:], lhsT=qT[:, t, :], rhs=kT[:, cols], start=True, stop=False)
                nc.tensor.matmul(out=s_ps[:], lhsT=ident_bf[:], rhs=live["minus", t][:, cols], start=False, stop=True)
                live["s_ps", t, b] = s_ps

        def row_max(t):
            bank_max = stats.tile([P, BANKS], F32, name="bank_max", tag="bank_max")
            for b in range(BANKS):
                nc.vector.tensor_reduce(
                    out=bank_max[:, b : b + 1], in_=live["s_ps", t, b][:], axis=AXIS.X, op=ALU.max
                )
            u_max = stats.tile([P, 1], F32, name="u_max", tag="u_max")
            nc.vector.tensor_reduce(out=u_max[:], in_=bank_max[:], axis=AXIS.X, op=ALU.max)
            live["u_max", t] = u_max

        def exponentials_from_psum(t):
            minus_max = stats.tile([P, 1], F32, name="minus_max", tag="minus_max")
            nc.scalar.mul(out=minus_max[:], in_=live["u_max", t][:], mul=-SCORE_SCALE)
            e = ring.tile([P, NODES], BF16, name="e", tag="e")
            bank_sums = stats.tile([P, BANKS], F32, name="bank_sums", tag="bank_sums")
            for b in range(BANKS):
                nc.scalar.activation(
                    out=e[:, BANK * b : BANK * (b + 1)],
                    in_=live["s_ps", t, b][:],
                    func=ACT.Exp,
                    bias=minus_max[:, 0:1],
                    scale=SCORE_SCALE,
                    accum_out=bank_sums[:, b : b + 1],
                )
            live["e", t] = e
            live["bank_sums", t] = bank_sums

        def total(t):
            nc.vector.tensor_reduce(out=row_sum(t), in_=live["bank_sums", t][:], axis=AXIS.X, op=ALU.add)

        def no_edge(t):
            first = away(t)[0]
            flags = ring.tile([P, BANKS * BANK // 2], BF16, name="flags", tag="flags")
            nc.vector.tensor_scalar(
                out=flags[:, : NODES - BANK * first],
                in0=adj_sb[:, t, BANK * first :],
                scalar1=0.0,
                scalar2=None,
                op0=ALU.is_equal,
            )
            live["flags", t] = flags

        def mask_away(t):
            if ("u", t) not in live:
                live["u", t] = ring.tile([P, NODES], F32, name="u", tag="u")
            for i, b in reversed(tuple(enumerate(away(t)))):
                raw = ring.tile([P, BANK], F32, name="raw", tag="raw")
                nc.scalar.copy(out=raw[:], in_=live["s_ps", t, b][:])
                nc.gpsimd.tensor_tensor(
                    out=live["u", t][:, BANK * b : BANK * (b + 1)],
                    in0=live["flags", t][:, BANK * i : BANK * (i + 1)],
                    in1=raw[:],
                    op=ALU.subtract,
                )

        def row_min(t):
            u_min = stats.tile([P, 1], F32, name="u_min", tag="u_min")
            nc.vector.tensor_reduce(out=u_min[:], in_=live["u", t][:], axis=AXIS.X, op=ALU.min)
            live["u_min", t] = u_min

        def exponentials(t):
            max_score = stats.tile([P, 1], F32, name="max_score", tag="max_score")
            nc.scalar.mul(out=max_score[:], in_=live["u_min", t][:], mul=SCORE_SCALE)
            e = ring.tile([P, NODES], BF16, name="e", tag="e")
            nc.scalar.activation(
                out=e[:],
                in_=live["u", t][:],
                func=ACT.Exp,
                bias=max_score[:, 0:1],
                scale=-SCORE_SCALE,
                accum_out=row_sum(t),
            )
            live["e", t] = e

        def transpose_e(t):
            e_words = live["e", t][:].bitcast(F32)
            for h in range(2):
                eT_ps = psum.tile([P, PACK, P], F32, name="eT_ps", tag="eT", bufs=2)
                for c in range(PACK):
                    chunk = PACK * h + c
                    nc.tensor.transpose(eT_ps[:, c, :], e_words[:, P * chunk : P * (chunk + 1)], ident_f32[:])
                live["eT_ps", t, h] = eT_ps

        def transpose_x(t):
            x_words = x_sb[:, t, :].bitcast(F32)
            xT_ps = psum.tile([P, 2, P], F32, name="xT_ps", tag="xT", bufs=1)
            for u in range(2):
                nc.tensor.transpose(xT_ps[:, u, :], x_words[:, P * u : P * (u + 1)], ident_f32[:])
            live["xT_ps", t] = xT_ps

        def regroup_e(t):
            e_grouped = ring.tile([P, PASSES, P, PACK], BF16, name="e_grouped", tag="e_grouped", align_bytes=64)
            for h in range(2):
                nc.scalar.copy(
                    out=e_grouped[:, 2 * h : 2 * h + 2, :, :].bitcast(F32),
                    in_=live["eT_ps", t, h][:].rearrange("p (g u) q -> p g q u", u=2),
                )
            live["e_grouped", t] = e_grouped

        def regroup_x(t, copy):
            x_grouped = ring.tile([P, P, PACK], BF16, name="x_grouped", tag="x_grouped", align_bytes=64)
            copy(out=x_grouped[:].bitcast(F32), in_=live["xT_ps", t][:].rearrange("p u q -> p q u"))
            live["x_grouped", t] = x_grouped

        def quantise_e(t):
            e_codes = ring.tile([P, PASSES * P], U32, name="e_codes", tag="e_codes", align_bytes=64)
            e_scales = ring.tile([P, PASSES * P], U8, name="e_scales", tag="e_scales", align_bytes=64)
            nc.vector.quantize_mx(
                out=e_codes[:].bitcast(FP8X4),
                scales=e_scales[:],
                in_=live["e_grouped", t][:].rearrange("p g q j -> p (g q j)"),
            )
            live["e_mx", t] = (e_codes, e_scales)

        def quantise_x(t):
            x_codes = ring.tile([P, P], U32, name="x_codes", tag="x_codes", align_bytes=64)
            x_scales = ring.tile([P, P], U8, name="x_scales", tag="x_scales", align_bytes=64)
            nc.vector.quantize_mx(
                out=x_codes[:].bitcast(FP8X4),
                scales=x_scales[:],
                in_=live["x_grouped", t][:].rearrange("p q j -> p (q j)"),
            )
            live["x_mx", t] = (x_codes, x_scales)

        def attend_pass(t, g):
            e_codes, e_scales = live["e_mx", t]
            cols = slice(P * g, P * (g + 1))
            nc.tensor.matmul_mx(
                out=live["acc", t // 2][:, t % 2, 0, :],
                lhsT=e_codes[:, cols].bitcast(FP8X4),
                lhsT_scale=e_scales[:, cols],
                rhs=v_codes[:, cols].bitcast(FP8X4),
                rhs_scale=v_scales[:, cols],
                start=(g == 0),
                stop=(g == PASSES - 1),
            )

        def project(t):
            x_codes, x_scales = live["x_mx", t]
            nc.tensor.matmul_mx(
                out=live["acc", t // 2][:, t % 2, 1, :],
                lhsT=x_codes[:].bitcast(FP8X4),
                lhsT_scale=x_scales[:],
                rhs=w_codes[:].bitcast(FP8X4),
                rhs_scale=w_scales[:],
                start=True,
                stop=True,
            )

        def attend(t):
            if t % 2 == 0:
                live["acc", t // 2] = psum.tile([P, 2, 2, D], F32, name="acc", tag="acc", bufs=1)
            for g in range(PASSES):
                attend_pass(t, g)
            project(t)

        def invert_sums(pair):
            inv_sums = stats.tile([P, 2], F32, name="inv_sums", tag="inv_sums")
            nc.vector.reciprocal(out=inv_sums[:], in_=live["row_sums", pair][:])
            live["inv_sums", pair] = inv_sums

        def out_of_psum(pair):
            acc = live["acc", pair]
            h = ring.tile([P, 2, D], F32, name="h", tag="h")
            skip = ring.tile([P, 2, D], F32, name="skip", tag="skip")
            h_sums = stats.tile([P, 2], F32, name="h_sums", tag="h_sums")
            skip_sums = stats.tile([P, 2], F32, name="skip_sums", tag="skip_sums")
            for i in range(2):
                nc.scalar.activation(
                    out=h[:, i, :],
                    in_=acc[:, i, 0, :],
                    func=ACT.Copy,
                    scale=live["inv_sums", pair][:, i : i + 1],
                    accum_out=h_sums[:, i : i + 1],
                )
                nc.scalar.activation(
                    out=skip[:, i, :], in_=acc[:, i, 1, :], func=ACT.Copy, accum_out=skip_sums[:, i : i + 1]
                )
            y_sums = stats.tile([P, 2], F32, name="y_sums", tag="y_sums")
            nc.gpsimd.tensor_tensor(out=y_sums[:], in0=h_sums[:], in1=skip_sums[:], op=ALU.add)
            neg_means = stats.tile([P, 2], F32, name="neg_means", tag="neg_means")
            nc.gpsimd.tensor_scalar(
                out=neg_means[:], in0=y_sums[:], scalar1=-1.0 / D, scalar2=0.0, op0=ALU.mult, op1=ALU.add
            )
            y = ring.tile([P, 2, D], F32, name="y", tag="y")
            nc.gpsimd.tensor_tensor(out=y[:], in0=h[:], in1=skip[:], op=ALU.add)
            live["y", pair] = y
            live["neg_means", pair] = neg_means

        def sum_squares(pair):
            squares = ring.tile([P, 2, D], F32, name="squares", tag="squares")
            sums_sq = stats.tile([P, 2], F32, name="sums_sq", tag="sums_sq")
            for i in range(2):
                nc.scalar.activation(
                    out=squares[:, i, :],
                    in_=live["y", pair][:, i, :],
                    func=ACT.Square,
                    bias=live["neg_means", pair][:, i : i + 1],
                    scale=1.0,
                    accum_out=sums_sq[:, i : i + 1],
                )
            live["sums_sq", pair] = sums_sq

        def normalise(pair):
            vars_eps = stats.tile([P, 2], F32, name="vars_eps", tag="vars_eps")
            nc.gpsimd.tensor_scalar(
                out=vars_eps[:],
                in0=live["sums_sq", pair][:],
                scalar1=1.0 / D,
                scalar2=LN_EPS,
                op0=ALU.mult,
                op1=ALU.add,
            )
            means = [live["neg_means", pair][:, i : i + 1] for i in range(2)]
            scale_and_store(pair, vars_eps, means, ALU.add)

        def scale_and_store(pair, vars_eps, means, centre_op):
            inv_stds = stats.tile([P, 2], F32, name="inv_stds", tag="inv_stds")
            nc.gpsimd.tensor_tensor(out=inv_stds[:], in0=vars_eps[:], in1=neg_half[:], op=ALU.pow)
            normed = ring.tile([P, 2, D], F32, name="normed", tag="normed")
            for i in range(2):
                nc.gpsimd.tensor_scalar(
                    out=normed[:, i, :],
                    in0=live["y", pair][:, i, :],
                    scalar1=means[i],
                    scalar2=inv_stds[:, i : i + 1],
                    op0=centre_op,
                    op1=ALU.mult,
                )
            scaled = ring.tile([P, 2, D], F32, name="scaled", tag="scaled")
            nc.gpsimd.tensor_tensor(
                out=scaled[:], in0=normed[:], in1=gain[:].unsqueeze(1).to_broadcast([P, 2, D]), op=ALU.mult
            )
            result = ring.tile([P, 2, D], F32, name="result", tag="result", bufs=3)
            nc.gpsimd.tensor_tensor(
                out=result[:], in0=scaled[:], in1=shift[:].unsqueeze(1).to_broadcast([P, 2, D]), op=ALU.add
            )
            nc.sync.dma_start(out=out_rows[:, 2 * pair : 2 * pair + 2, :], in_=result[:])

        stack.enter_context(tc.manual_schedule())
        transpose_keys(0)
        transpose_queries(0)
        queries_out(0, 0, 1)
        for b in range(1, BANKS):
            transpose_keys(b)
        queries_out(0, 1, 4)
        scores(0, kept(0))
        last = TILES - 1
        for r in range(TILES):
            if r != TENSOR_MASKED:
                mask(r, kept(r))
            if r + 2 == last:
                minus_no_edge(last)
            if r < last and away(r + 1):
                no_edge(r + 1)
            if r + 1 == last:
                masked_scores(last)
            elif r < last:
                scores(r + 1, away(r + 1)[::-1] + kept(r + 1))
            if r < last:
                transpose_x(r)
            if r >= 1:
                exponentials(r - 1)
            if r < last:
                mask_away(r + 1)
            if r == 0:
                regroup_weights()
            if r >= 4 and r % 2 == 0:
                out_of_psum((r - 4) // 2)
            if r >= 5 and r % 2 == 1:
                sum_squares((r - 5) // 2)
                normalise((r - 5) // 2)
            if r < last - 1:
                regroup_x(r, nc.scalar.copy)
            if r in (2, 6, 10):
                transpose_queries((r + 2) // 4)
                queries_out((r + 2) // 4, 0, 4)
            if 1 <= r < last:
                transpose_e(r - 1)
                regroup_e(r - 1)
            if r == 2:
                quantise_weights()
            if r >= 3 and r % 2 == 1:
                invert_sums((r - 3) // 2)
            if r >= 2:
                quantise_e(r - 2)
                quantise_x(r - 2)
                attend(r - 2)
            if r == last:
                transpose_e(last - 1)
                regroup_e(last - 1)
                regroup_x(last - 1, nc.vector.tensor_copy)
                transpose_x(last)
                quantise_x(last - 1)
            if r == TENSOR_MASKED:
                row_max(r)
            else:
                row_min(r)

        def pair_streams(pair):
            acc = live["acc", pair]
            skip = ring.tile([P, 2, D], F32, name="skip", tag="skip")
            nc.vector.tensor_copy(out=skip[:], in_=acc[:, :, 1, :])
            y = ring.tile([P, 2, D], F32, name="y", tag="y")
            for i in range(2):
                nc.vector.scalar_tensor_tensor(
                    out=y[:, i, :],
                    in0=acc[:, i, 0, :],
                    scalar=live["inv_sums", pair][:, i : i + 1],
                    in1=skip[:, i, :],
                    op0=ALU.mult,
                    op1=ALU.add,
                )
            live["y", pair] = y

        def pair_moments(pair):
            parts = stats.tile([P, 2, 6], F32, name="parts", tag="parts")
            for i in range(2):
                nc.vector.bn_stats(out=parts[:, i, :], in_=live["y", pair][:, i, :])
            mean_vars = stats.tile([P, 2, 2], F32, name="mean_vars", tag="mean_vars")
            for i in range(2):
                nc.vector.bn_aggr(out=mean_vars[:, i, :], in_=parts[:, i, :])
            live["mean_vars", pair] = mean_vars

        t14 = last - 1
        pair_streams(t14 // 2 - 1)
        quantise_e(t14)
        regroup_x(last, nc.vector.tensor_copy)
        quantise_x(last)
        pair_moments(t14 // 2 - 1)
        attend(t14)
        project(last)

        exponentials_from_psum(last)
        e_words = live["e", last][:].bitcast(F32)
        e_grouped = ring.tile([P, PASSES, P, PACK], BF16, name="e_grouped", tag="e_grouped", align_bytes=64)
        e_codes = ring.tile([P, PASSES * P], U32, name="e_codes", tag="e_codes", align_bytes=64)
        e_scales = ring.tile([P, PASSES * P], U8, name="e_scales", tag="e_scales", align_bytes=64)
        live["e_mx", last] = (e_codes, e_scales)

        def normalise_last_pair(pair):
            mean_vars = live["mean_vars", pair]
            vars_eps = stats.tile([P, 2], F32, name="vars_eps", tag="vars_eps")
            nc.gpsimd.tensor_scalar(
                out=vars_eps[:], in0=mean_vars[:, :, 1], scalar1=1.0, scalar2=LN_EPS, op0=ALU.mult, op1=ALU.add
            )
            scale_and_store(pair, vars_eps, [mean_vars[:, i, 0:1] for i in range(2)], ALU.subtract)

        def last_transposes(g):
            if g < 2:
                eT_ps = psum.tile([P, 2, P], F32, name="eT_last", tag="eT", bufs=2)
            else:
                eT_ps = psum.tile([P, 2, P], F32, name="eT_last", tag="scores", bufs=BANKS)
            for u in range(2):
                chunk = 2 * g + u
                nc.tensor.transpose(eT_ps[:, u, :], e_words[:, P * chunk : P * (chunk + 1)], ident_f32[:])
            live["eT_ps", last, g] = eT_ps

        def last_regroup(g, copy):
            copy(
                out=e_grouped[:, g, :, :].bitcast(F32),
                in_=live["eT_ps", last, g][:].rearrange("p u q -> p q u"),
            )

        def last_quantise(g, passes):
            cols = slice(P * g, P * (g + passes))
            nc.vector.quantize_mx(
                out=e_codes[:, cols].bitcast(FP8X4),
                scales=e_scales[:, cols],
                in_=e_grouped[:, g : g + passes, :, :].rearrange("p g q j -> p (g q j)"),
            )

        def last_skips():
            skips = ring.tile([P, 2, D], F32, name="skip", tag="skip")
            nc.vector.tensor_copy(out=skips[:], in_=live["acc", last // 2][:, :, 1, :])
            live["skips"] = skips

        def invert(t):
            inv_sum = stats.tile([P, 1], F32, name="inv_sum", tag="inv_sum")
            nc.vector.reciprocal(out=inv_sum[:], in_=row_sum(t))
            live["inv_sum", t] = inv_sum

        def add_streams(t):
            y = ring.tile([P, D], F32, name="y", tag="y")
            nc.vector.scalar_tensor_tensor(
                out=y[:],
                in0=live["acc", t // 2][:, t % 2, 0, :],
                scalar=live["inv_sum", t][:, 0:1],
                in1=live["skips"][:, t % 2, :],
                op0=ALU.mult,
                op1=ALU.add,
            )
            live["y", t] = y

        def moments(t):
            parts = stats.tile([P, 6], F32, name="parts", tag="parts")
            nc.vector.bn_stats(out=parts[:], in_=live["y", t][:])
            mean_var = stats.tile([P, 2], F32, name="mean_var", tag="mean_var")
            nc.vector.bn_aggr(out=mean_var[:], in_=parts[:])
            live["mean_var", t] = mean_var

        def inverse_deviation(t):
            inv_std = stats.tile([P, 1], F32, name="inv_std", tag="inv_std")
            nc.scalar.activation(
                out=inv_std[:],
                in_=live["mean_var", t][:, 1:2],
                func=ACT.Abs_reciprocal_sqrt,
                bias=LN_EPS,
                scale=1.0,
            )
            live["inv_std", t] = inv_std

        def centre(t):
            centred = ring.tile([P, D], F32, name="centred", tag="normed")
            nc.vector.scalar_tensor_tensor(
                out=centred[:],
                in0=live["y", t][:],
                scalar=live["mean_var", t][:, 0:1],
                in1=gain[:],
                op0=ALU.subtract,
                op1=ALU.mult,
            )
            live["centred", t] = centred

        def finish(t):
            result = ring.tile([P, D], F32, name="result_last", tag="result", bufs=3)
            nc.vector.scalar_tensor_tensor(
                out=result[:],
                in0=live["centred", t][:],
                scalar=live["inv_std", t][:, 0:1],
                in1=shift[:],
                op0=ALU.mult,
                op1=ALU.add,
            )
            nc.sync.dma_start(out=out_rows[:, t, :], in_=result[:])

        normalise_last_pair(t14 // 2 - 1)
        for g in range(PASSES):
            last_transposes(g)
        invert(t14)
        last_skips()
        last_regroup(0, nc.vector.tensor_copy)
        add_streams(t14)
        last_regroup(1, nc.vector.tensor_copy)
        last_regroup(2, nc.scalar.copy)
        last_quantise(0, 2)
        attend_pass(last, 0)
        attend_pass(last, 1)
        total(last)
        last_regroup(3, nc.vector.tensor_copy)
        last_quantise(2, 1)
        invert(last)
        last_quantise(3, 1)
        attend_pass(last, 2)
        attend_pass(last, 3)
        moments(t14)
        inverse_deviation(t14)
        add_streams(last)
        centre(t14)
        moments(last)
        inverse_deviation(last)
        finish(t14)
        centre(last)
        finish(last)
